import numpy as np
import ml_dtypes


def mxq(x, axis, fmt="e4m3"):
    dtype, down = {"e4m3": (ml_dtypes.float8_e4m3fn, 7), "e5m2": (ml_dtypes.float8_e5m2, 14)}[fmt]
    v = np.moveaxis(np.asarray(x, np.float32).astype(ml_dtypes.bfloat16).astype(np.float64), axis, -1)
    blocks = v.reshape(v.shape[:-1] + (-1, 32))
    amax = np.abs(blocks).max(-1, keepdims=True)
    byte = np.maximum(np.where(amax > 0, np.frexp(amax)[1] - 1 + 127, 0) - down, 1)
    scale = np.exp2(byte - 127.0)
    codes = (blocks / scale).astype(np.float32).astype(dtype).astype(np.float64)
    return np.moveaxis((codes * scale).reshape(v.shape), -1, axis)


WIDE = False


def mx_kscale(k):
    if not WIDE:
        return np.ones(k)
    levels = np.array([10, -10, 5, -5, 0])
    a = np.random.permutation(np.resize(levels, k // 512 * 4)).reshape(k // 512, 4)
    idx = np.arange(k)
    return np.exp2(a[idx // 512, idx % 128 // 32])


BF16 = ml_dtypes.bfloat16


def bf(x):
    return np.asarray(x, np.float32).astype(BF16)


def f64(x):
    return np.asarray(x).astype(np.float64)


B, E, S, H = 16, 512, 512, 8
DH = E // H


def setup_inputs():
    s = mx_kscale(S)
    return {"x_proj": bf(np.random.standard_normal((B, S, E)) * s[None, :, None]),
            "mix_mat": bf(np.random.standard_normal((H, S, S)) * np.sqrt(2.0 / S) / s[None, :, None]),
            "mix_b": bf(np.random.standard_normal((H, S)) * 0.2),
            "out_w": bf(np.random.standard_normal((E, E)) / np.sqrt(E)),
            "out_b": bf(np.random.standard_normal(E) * 0.2)}


def reference(x_proj, mix_mat, mix_b, out_w, out_b):
    p = f64(x_proj).reshape(B, S, H, DH).transpose(0, 2, 3, 1)
    idx = np.arange(S)
    keep = idx[None, :] >= idx[:, None]
    wm = np.where(keep[None], f64(mix_mat), 0.0)
    mixed = (mxq(p, 3, "e4m3") @ mxq(wm, 1, "e4m3")) + f64(mix_b)[None, :, None, :]
    y = mixed.transpose(0, 3, 1, 2).reshape(B, S, E)
    out = (mxq(y, 2, "e4m3") @ mxq(f64(out_w), 1, "e4m3").T) + f64(out_b)
    return out.transpose(0, 2, 1)

@@ -1,0 +1,178 @@
+from contextlib import ExitStack
+
+import concourse.mybir as mybir
+from concourse.masks import make_identity
+
+BF16 = mybir.dt.bfloat16
+F32 = mybir.dt.float32
+I32 = mybir.dt.int32
+U32 = mybir.dt.uint32
+U8 = mybir.dt.uint8
+FP8X4 = mybir.dt.float8_e4m3fn_x4
+ALU = mybir.AluOpType
+ACT = mybir.ActivationFunctionType
+
+P = 128
+B, S, E, H = 16, 512, 512, 8
+FLOPS = 2 * 2 * B * S * S * E
+
+XQ_W = 768
+XQ_BUFS = 4
+X_PIECES = ((0, 0, 64), (128, 64, 128), (320, 192, 128), (512, 320, 128), (704, 448, 64))
+XRAW_BUFS = 8
+XG_BUFS = 10
+
+
+def tile_mixerblock_pa_t_kernel(tc, x_proj, mix_mat, mix_b, out_w, out_b, out):
+    nc = tc.nc
+    with ExitStack() as ctx:
+        const = ctx.enter_context(tc.tile_pool(name="const", bufs=1))
+        xpool = ctx.enter_context(tc.tile_pool(name="xraw", bufs=XRAW_BUFS))
+        xgpool = ctx.enter_context(tc.tile_pool(name="xgrouped", bufs=XG_BUFS))
+        wgpool = ctx.enter_context(tc.tile_pool(name="wgrouped", bufs=4))
+        ypool = ctx.enter_context(tc.tile_pool(name="y", bufs=3))
+        opool = ctx.enter_context(tc.tile_pool(name="outs", bufs=6))
+        psum1 = ctx.enter_context(tc.psum_pool(name="psum1", bufs=4))
+        psum2 = ctx.enter_context(tc.psum_pool(name="psum2", bufs=4))
+        ctx.enter_context(tc.manual_schedule())
+
+        bias_raw = const.tile([P, 4, S], BF16, name="bias_raw")
+        bias_g = const.tile([P, S, 4], BF16, name="bias_g")
+        outb_raw = const.tile([P, 4], BF16, name="outb_raw")
+        outb = const.tile([P, 4], F32, name="outb")
+        wr = const.tile([P, H, 4, S], BF16, name="wr")
+        wq = const.tile([P, H, S], U32, name="wq", align_bytes=64)
+        ws = const.tile([P, H, S], U8, name="ws", align_bytes=64)
+        ow = const.tile([P, 4, E], BF16, name="ow")
+        owg = const.tile([P, 4, P, 4], BF16, name="owg", align_bytes=64)
+        owq = const.tile([P, 4 * P], U32, name="owq", align_bytes=64)
+        ows = const.tile([P, 4 * P], U8, name="ows", align_bytes=64)
+        tri_f = const.tile([P, P], F32, name="tri_f")
+        tri = const.tile([P, P], BF16, name="tri")
+        ident = const.tile([P, P], BF16, name="ident")
+        xq = [const.tile([P, XQ_W], U32, name="xq%d" % k, align_bytes=64) for k in range(XQ_BUFS)]
+        xs = [const.tile([P, XQ_W], U8, name="xs%d" % k, align_bytes=64) for k in range(XQ_BUFS)]
+        xraw = {}
+        xg = {}
+        wmg = {}
+        ps1 = {}
+        yg = {}
+
+        def load_x(b):
+            xraw[b] = xpool.tile([P, 4, E], BF16, name="xr", tag="xr")
+            nc.sync.dma_start(out=xraw[b][:], in_=x_proj[b].rearrange("(j p) c -> p j c", p=P))
+
+        def load_w(g, j):
+            nc.sync.dma_start(out=wr[:, 4 * g:4 * g + 4, j, P * j:S],
+                              in_=mix_mat[4 * g:4 * g + 4, P * j:P * (j + 1), P * j:S].rearrange("h p s -> p h s"))
+
+        def group(engine_copy, dst, src):
+            engine_copy(out=dst.rearrange("p (c i) t -> p c t i", i=4), in_=src.rearrange("p t (c i) -> p c t i", i=4))
+
+        def group_x(b):
+            xg[b] = xgpool.tile([P, E, 4], BF16, name="xg", tag="xg", align_bytes=64)
+            group(nc.scalar.copy, xg[b][:], xraw[b][:])
+            if b + XRAW_BUFS < B:
+                load_x(b + XRAW_BUFS)
+
+        def quantise_x(b):
+            for (w0, c0, n) in X_PIECES:
+                nc.vector.quantize_mx(out=xq[b % XQ_BUFS][:, w0:w0 + n].bitcast(FP8X4),
+                                      scales=xs[b % XQ_BUFS][:, w0:w0 + n],
+                                      in_=xg[b][:, c0:c0 + n, :].rearrange("p c j -> p (c j)"))
+
+        def mix(b, i):
+            cols = slice(P * i, P * (i + 1))
+            ps1[(b, i)] = psum1.tile([P, 4, P], F32, name="ps1", tag="s1")
+            for hp in range(4):
+                for h2 in range(2):
+                    w0 = 192 * hp + 64 * h2
+                    nc.tensor.matmul_mx(out=ps1[(b, i)][:, hp, :],
+                                        lhsT=xq[b % XQ_BUFS][:, w0:w0 + P].bitcast(FP8X4),
+                                        lhsT_scale=xs[b % XQ_BUFS][:, w0:w0 + P],
+                                        rhs=wq[:, 2 * hp + h2, cols].bitcast(FP8X4),
+                                        rhs_scale=ws[:, 2 * hp + h2, cols],
+                                        start=(h2 == 0), stop=(h2 == 1))
+
+        def add_mix_bias(b, i):
+            cols = slice(P * i, P * (i + 1))
+            nc.vector.tensor_tensor(out=yg[b][:, cols, :], in0=ps1[(b, i)][:].rearrange("p j s -> p s j"),
+                                    in1=bias_g[:, cols, :], op=ALU.add)
+
+        mb = mix_b.rearrange("(hp h2) s -> h2 hp s", h2=2)
+        for h2 in range(2):
+            nc.scalar.dma_start(out=bias_raw[64 * h2:64 * h2 + 64, :, :], in_=mb[h2].partition_broadcast(64))
+        nc.scalar.dma_start(out=outb_raw[:], in_=out_b.rearrange("(m r) -> m r", r=4))
+        load_x(0)
+        for j in range(4):
+            load_w(0, j)
+        load_x(1)
+        for j in range(4):
+            load_w(1, j)
+        load_x(2)
+        nc.sync.dma_start(out=ow[:], in_=out_w.rearrange("(m r) c -> m r c", r=4))
+        for b in range(3, XRAW_BUFS):
+            load_x(b)
+
+        nc.gpsimd.memset(tri_f[:], 1.0)
+        nc.gpsimd.affine_select(out=tri_f[:], in_=tri_f[:], pattern=[[1, P]], compare_op=ALU.is_ge,
+                                fill=0.0, base=0, channel_multiplier=-1)
+        make_identity(nc, ident[:])
+        nc.gpsimd.tensor_scalar(out=bias_g[:], in0=bias_raw[:].rearrange("p j s -> p s j"), scalar1=1.0, scalar2=0.0,
+                                op0=ALU.mult, op1=ALU.add)
+        for j in range(1, 4):
+            nc.vector.memset(wr[:, :, j, 0:P * j], 0.0)
+        for k in range(XQ_BUFS):
+            nc.vector.memset(xq[k][:].bitcast(I32), 0)
+            nc.vector.memset(xs[k][:].bitcast(I32), 0)
+        nc.vector.tensor_copy(out=tri[:], in_=tri_f[:])
+        nc.vector.tensor_copy(out=outb[:], in_=outb_raw[:])
+
+        for g in range(2):
+            group_x(g)
+            for j in range(4):
+                diag = wr[:, 4 * g:4 * g + 4, j, P * j:P * (j + 1)]
+                nc.vector.tensor_tensor(out=diag, in0=diag, in1=tri[:].unsqueeze(1).to_broadcast([P, 4, P]), op=ALU.mult)
+            for h in range(4 * g, 4 * g + 4):
+                wmg[h] = wgpool.tile([P, S, 4], BF16, name="wmg", tag="wmg", align_bytes=64)
+                group(nc.scalar.copy if h % 4 == 3 else nc.vector.tensor_copy, wmg[h][:], wr[:, h])
+            quantise_x(g)
+            for h in range(4 * g, 4 * g + 4):
+                nc.vector.quantize_mx(out=wq[:, h, :].bitcast(FP8X4), scales=ws[:, h, :],
+                                      in_=wmg[h][:].rearrange("p s j -> p (s j)"))
+        group_x(2)
+        for r in range(4):
+            pst = psum2.tile([P, 4, P], BF16, name="pst", tag="s2")
+            for j in range(4):
+                nc.tensor.transpose(pst[:, j, :], ow[:, r, P * j:P * (j + 1)], ident[:])
+            nc.scalar.copy(out=owg[:, r, :, :], in_=pst[:].rearrange("p j m -> p m j"))
+        for b in range(3, XG_BUFS):
+            group_x(b)
+        nc.vector.quantize_mx(out=owq[:].bitcast(FP8X4), scales=ows[:], in_=owg[:].rearrange("p r m j -> p (r m j)"))
+        for i in range(4):
+            mix(0, i)
+
+        for b in range(B):
+            if b % 2 == 0 and XG_BUFS + b // 2 < B:
+                group_x(XG_BUFS + b // 2)
+            yg[b] = ypool.tile([P, S, 4], BF16, name="yg", tag="yg", align_bytes=64)
+            for i in range(4):
+                add_mix_bias(b, i)
+                if b + 1 < B:
+                    mix(b + 1, i)
+            if b + 2 < B:
+                quantise_x(b + 2)
+            yq = ypool.tile([P, S], U32, name="yq", tag="yq", align_bytes=64)
+            ys = ypool.tile([P, S], U8, name="ys", tag="ys", align_bytes=64)
+            nc.vector.quantize_mx(out=yq[:].bitcast(FP8X4), scales=ys[:], in_=yg[b][:].rearrange("p s j -> p (s j)"))
+            rows = out[b].rearrange("(m r) s -> m r s", r=4)
+            for half in range(2):
+                ob = opool.tile([P, 2, S], F32, name="ob", tag="ob")
+                for k in range(2):
+                    r = 2 * half + k
+                    ps2 = psum2.tile([P, S], F32, name="ps2", tag="s2")
+                    nc.tensor.matmul_mx(out=ps2[:], lhsT=owq[:, P * r:P * (r + 1)].bitcast(FP8X4),
+                                        lhsT_scale=ows[:, P * r:P * (r + 1)],
+                                        rhs=yq[:].bitcast(FP8X4), rhs_scale=ys[:], start=True, stop=True)
+                    nc.scalar.activation(out=ob[:, k, :], in_=ps2[:], func=ACT.Identity, bias=outb[:, r:r + 1], scale=1.0)
+                nc.scalar.dma_start(out=rows[:, 2 * half:2 * half + 2, :], in_=ob[:])

@@ -18,9 +18,12 @@ FLOPS = 2 * 2 * B * S * S * E
 
 XQ_W = 768
 XQ_BUFS = 4
-X_PIECES = ((0, 0, 64), (128, 64, 128), (320, 192, 128), (512, 320, 128), (704, 448, 64))
+C_S = 192
+X_PIECES_S = ((0, 0, 64), (128, 64, 128))
+X_PIECES_G = ((320, 0, 128), (512, 128, 128), (704, 256, 64))
 XRAW_BUFS = 8
-XG_BUFS = 10
+XS_BUFS = 6
+XG_BUFS = 3
 
 
 def tile_mixerblock_pa_t_kernel(tc, x_proj, mix_mat, mix_b, out_w, out_b, out):
@@ -28,7 +31,8 @@ def tile_mixerblock_pa_t_kernel(tc, x_proj, mix_mat, mix_b, out_w, out_b, out):
     with ExitStack() as ctx:
         const = ctx.enter_context(tc.tile_pool(name="const", bufs=1))
         xpool = ctx.enter_context(tc.tile_pool(name="xraw", bufs=XRAW_BUFS))
-        xgpool = ctx.enter_context(tc.tile_pool(name="xgrouped", bufs=XG_BUFS))
+        xspool = ctx.enter_context(tc.tile_pool(name="xgrouped_s", bufs=XS_BUFS))
+        xgpool = ctx.enter_context(tc.tile_pool(name="xgrouped_g", bufs=XG_BUFS))
         wgpool = ctx.enter_context(tc.tile_pool(name="wgrouped", bufs=4))
         ypool = ctx.enter_context(tc.tile_pool(name="y", bufs=3))
         opool = ctx.enter_context(tc.tile_pool(name="outs", bufs=6))
@@ -53,7 +57,8 @@ def tile_mixerblock_pa_t_kernel(tc, x_proj, mix_mat, mix_b, out_w, out_b, out):
         xq = [const.tile([P, XQ_W], U32, name="xq%d" % k, align_bytes=64) for k in range(XQ_BUFS)]
         xs = [const.tile([P, XQ_W], U8, name="xs%d" % k, align_bytes=64) for k in range(XQ_BUFS)]
         xraw = {}
-        xg = {}
+        xg_s = {}
+        xg_g = {}
         wmg = {}
         ps1 = {}
         yg = {}
@@ -69,17 +74,30 @@ def tile_mixerblock_pa_t_kernel(tc, x_proj, mix_mat, mix_b, out_w, out_b, out):
         def group(engine_copy, dst, src):
             engine_copy(out=dst.rearrange("p (c i) t -> p c t i", i=4), in_=src.rearrange("p t (c i) -> p c t i", i=4))
 
-        def group_x(b):
-            xg[b] = xgpool.tile([P, E, 4], BF16, name="xg", tag="xg", align_bytes=64)
-            group(nc.scalar.copy, xg[b][:], xraw[b][:])
-            if b + XRAW_BUFS < B:
-                load_x(b + XRAW_BUFS)
+        def group_x_s(b):
+            xg_s[b] = xspool.tile([P, C_S, 4], BF16, name="xg_s", tag="xg_s", align_bytes=64)
+            group(nc.scalar.copy, xg_s[b][:], xraw[b][:, :, 0:C_S])
+
+        def new_xg_g(b):
+            xg_g[b] = xgpool.tile([P, E - C_S, 4], BF16, name="xg_g", tag="xg_g", align_bytes=64)
+
+        def group_x_g(b):
+            if b >= XG_BUFS:
+                new_xg_g(b)
+            if b < XG_BUFS:
+                group(nc.scalar.copy, xg_g[b][:], xraw[b][:, :, C_S:E])
+            else:
+                nc.gpsimd.tensor_scalar(out=xg_g[b][:], in0=xraw[b][:, :, C_S:E].rearrange("p t c -> p c t"),
+                                        scalar1=1.0, scalar2=0.0, op0=ALU.mult, op1=ALU.add)
 
         def quantise_x(b):
-            for (w0, c0, n) in X_PIECES:
-                nc.vector.quantize_mx(out=xq[b % XQ_BUFS][:, w0:w0 + n].bitcast(FP8X4),
-                                      scales=xs[b % XQ_BUFS][:, w0:w0 + n],
-                                      in_=xg[b][:, c0:c0 + n, :].rearrange("p c j -> p (c j)"))
+            for (pieces, src) in ((X_PIECES_S, xg_s[b]), (X_PIECES_G, xg_g[b])):
+                for (w0, c0, n) in pieces:
+                    nc.vector.quantize_mx(out=xq[b % XQ_BUFS][:, w0:w0 + n].bitcast(FP8X4),
+                                          scales=xs[b % XQ_BUFS][:, w0:w0 + n],
+                                          in_=src[:, c0:c0 + n, :].rearrange("p c j -> p (c j)"))
+            if b + XG_BUFS < B:
+                group_x_g(b + XG_BUFS)
 
         def mix(b, i):
             cols = slice(P * i, P * (i + 1))
@@ -128,33 +146,39 @@ def tile_mixerblock_pa_t_kernel(tc, x_proj, mix_mat, mix_b, out_w, out_b, out):
         nc.vector.tensor_copy(out=tri[:], in_=tri_f[:])
         nc.vector.tensor_copy(out=outb[:], in_=outb_raw[:])
 
+        for b in range(XG_BUFS):
+            new_xg_g(b)
+
         for g in range(2):
-            group_x(g)
+            group_x_s(g)
+            group_x_g(g)
             for j in range(4):
                 diag = wr[:, 4 * g:4 * g + 4, j, P * j:P * (j + 1)]
                 nc.vector.tensor_tensor(out=diag, in0=diag, in1=tri[:].unsqueeze(1).to_broadcast([P, 4, P]), op=ALU.mult)
             for h in range(4 * g, 4 * g + 4):
                 wmg[h] = wgpool.tile([P, S, 4], BF16, name="wmg", tag="wmg", align_bytes=64)
-                group(nc.scalar.copy if h % 4 == 3 else nc.vector.tensor_copy, wmg[h][:], wr[:, h])
+                group(nc.scalar.copy if h % 2 == 1 else nc.vector.tensor_copy, wmg[h][:], wr[:, h])
             quantise_x(g)
             for h in range(4 * g, 4 * g + 4):
                 nc.vector.quantize_mx(out=wq[:, h, :].bitcast(FP8X4), scales=ws[:, h, :],
                                       in_=wmg[h][:].rearrange("p s j -> p (s j)"))
-        group_x(2)
+        group_x_s(2)
+        group_x_g(2)
         for r in range(4):
             pst = psum2.tile([P, 4, P], BF16, name="pst", tag="s2")
             for j in range(4):
                 nc.tensor.transpose(pst[:, j, :], ow[:, r, P * j:P * (j + 1)], ident[:])
             nc.scalar.copy(out=owg[:, r, :, :], in_=pst[:].rearrange("p j m -> p m j"))
-        for b in range(3, XG_BUFS):
-            group_x(b)
-        nc.vector.quantize_mx(out=owq[:].bitcast(FP8X4), scales=ows[:], in_=owg[:].rearrange("p r m j -> p (r m j)"))
+        for b in range(3, XS_BUFS):
+            group_x_s(b)
         for i in range(4):
             mix(0, i)
 
         for b in range(B):
-            if b % 2 == 0 and XG_BUFS + b // 2 < B:
-                group_x(XG_BUFS + b // 2)
+            if b + XRAW_BUFS < B:
+                load_x(b + XRAW_BUFS)
+            if b + XS_BUFS < B:
+                group_x_s(b + XS_BUFS)
             yg[b] = ypool.tile([P, S, 4], BF16, name="yg", tag="yg", align_bytes=64)
             for i in range(4):
                 add_mix_bias(b, i)
@@ -162,6 +186,9 @@ def tile_mixerblock_pa_t_kernel(tc, x_proj, mix_mat, mix_b, out_w, out_b, out):
                     mix(b + 1, i)
             if b + 2 < B:
                 quantise_x(b + 2)
+            if b == 0:
+                nc.vector.quantize_mx(out=owq[:].bitcast(FP8X4), scales=ows[:],
+                                      in_=owg[:].rearrange("p r m j -> p (r m j)"))
             yq = ypool.tile([P, S], U32, name="yq", tag="yq", align_bytes=64)
             ys = ypool.tile([P, S], U8, name="ys", tag="ys", align_bytes=64)
             nc.vector.quantize_mx(out=yq[:].bitcast(FP8X4), scales=ys[:], in_=yg[b][:].rearrange("p s j -> p (s j)"))

@@ -52,7 +52,7 @@ def tile_mixerblock_pa_t_kernel(tc, x_proj, mix_mat, mix_b, out_w, out_b, out):
         owq = const.tile([P, 4 * P], U32, name="owq", align_bytes=64)
         ows = const.tile([P, 4 * P], U8, name="ows", align_bytes=64)
         tri_f = const.tile([P, P], F32, name="tri_f")
-        tri = const.tile([P, P], BF16, name="tri")
+        tri = const.tile([P, 4, P], BF16, name="tri")
         ident = const.tile([P, P], BF16, name="ident")
         xq = [const.tile([P, XQ_W], U32, name="xq%d" % k, align_bytes=64) for k in range(XQ_BUFS)]
         xs = [const.tile([P, XQ_W], U8, name="xs%d" % k, align_bytes=64) for k in range(XQ_BUFS)]
@@ -141,9 +141,9 @@ def tile_mixerblock_pa_t_kernel(tc, x_proj, mix_mat, mix_b, out_w, out_b, out):
         for j in range(1, 4):
             nc.vector.memset(wr[:, :, j, 0:P * j], 0.0)
         for k in range(XQ_BUFS):
-            nc.vector.memset(xq[k][:].bitcast(I32), 0)
-            nc.vector.memset(xs[k][:].bitcast(I32), 0)
-        nc.vector.tensor_copy(out=tri[:], in_=tri_f[:])
+            nc.vector.memset(xq[k][:].bitcast(I32).rearrange("p (g w) -> p g w", g=4)[:, :, 64:128], 0)
+            nc.vector.memset(xs[k][:].bitcast(I32).rearrange("p (g w) -> p g w", g=4)[:, :, 16:32], 0)
+        nc.vector.tensor_copy(out=tri[:], in_=tri_f[:].unsqueeze(1).to_broadcast([P, 4, P]))
         nc.vector.tensor_copy(out=outb[:], in_=outb_raw[:])
 
         for b in range(XG_BUFS):
@@ -154,7 +154,7 @@ def tile_mixerblock_pa_t_kernel(tc, x_proj, mix_mat, mix_b, out_w, out_b, out):
             group_x_g(g)
             for j in range(4):
                 diag = wr[:, 4 * g:4 * g + 4, j, P * j:P * (j + 1)]
-                nc.vector.tensor_tensor(out=diag, in0=diag, in1=tri[:].unsqueeze(1).to_broadcast([P, 4, P]), op=ALU.mult)
+                nc.vector.tensor_tensor(out=diag, in0=diag, in1=tri[:], op=ALU.mult)
             for h in range(4 * g, 4 * g + 4):
                 wmg[h] = wgpool.tile([P, S, 4], BF16, name="wmg", tag="wmg", align_bytes=64)
                 group(nc.scalar.copy if h % 2 == 1 else nc.vector.tensor_copy, wmg[h][:], wr[:, h])
@@ -193,6 +193,7 @@ def tile_mixerblock_pa_t_kernel(tc, x_proj, mix_mat, mix_b, out_w, out_b, out):
             ys = ypool.tile([P, S], U8, name="ys", tag="ys", align_bytes=64)
             nc.vector.quantize_mx(out=yq[:].bitcast(FP8X4), scales=ys[:], in_=yg[b][:].rearrange("p s j -> p (s j)"))
             rows = out[b].rearrange("(m r) s -> m r s", r=4)
+            last = b == B - 1
             for half in range(2):
                 ob = opool.tile([P, 2, S], F32, name="ob", tag="ob")
                 for k in range(2):
@@ -201,5 +202,13 @@ def tile_mixerblock_pa_t_kernel(tc, x_proj, mix_mat, mix_b, out_w, out_b, out):
                     nc.tensor.matmul_mx(out=ps2[:], lhsT=owq[:, P * r:P * (r + 1)].bitcast(FP8X4),
                                         lhsT_scale=ows[:, P * r:P * (r + 1)],
                                         rhs=yq[:].bitcast(FP8X4), rhs_scale=ys[:], start=True, stop=True)
-                    nc.scalar.activation(out=ob[:, k, :], in_=ps2[:], func=ACT.Identity, bias=outb[:, r:r + 1], scale=1.0)
-                nc.scalar.dma_start(out=rows[:, 2 * half:2 * half + 2, :], in_=ob[:])
+                    if last and k == 1:
+                        nc.vector.tensor_scalar_add(out=ob[:, k, :], in0=ps2[:], scalar1=outb[:, r:r + 1])
+                        nc.sync.dma_start(out=rows[:, r:r + 1, :], in_=ob[:, k:k + 1, :])
+                    else:
+                        nc.scalar.activation(out=ob[:, k, :], in_=ps2[:], func=ACT.Identity, bias=outb[:, r:r + 1],
+                                             scale=1.0)
+                        if last:
+                            nc.scalar.dma_start(out=rows[:, r:r + 1, :], in_=ob[:, k:k + 1, :])
+                if not last:
+                    nc.scalar.dma_start(out=rows[:, 2 * half:2 * half + 2, :], in_=ob[:])

@@ -52,7 +52,8 @@ def tile_mixerblock_pa_t_kernel(tc, x_proj, mix_mat, mix_b, out_w, out_b, out):
         owq = const.tile([P, 4 * P], U32, name="owq", align_bytes=64)
         ows = const.tile([P, 4 * P], U8, name="ows", align_bytes=64)
         tri_f = const.tile([P, P], F32, name="tri_f")
-        tri = const.tile([P, 4, P], BF16, name="tri")
+        tri = const.tile([P, P], BF16, name="tri")
+        spread = const.tile([P, P // 2], I32, name="spread")
         ident = const.tile([P, P], BF16, name="ident")
         xq = [const.tile([P, XQ_W], U32, name="xq%d" % k, align_bytes=64) for k in range(XQ_BUFS)]
         xs = [const.tile([P, XQ_W], U8, name="xs%d" % k, align_bytes=64) for k in range(XQ_BUFS)]
@@ -143,7 +144,11 @@ def tile_mixerblock_pa_t_kernel(tc, x_proj, mix_mat, mix_b, out_w, out_b, out):
         for k in range(XQ_BUFS):
             nc.vector.memset(xq[k][:].bitcast(I32).rearrange("p (g w) -> p g w", g=4)[:, :, 64:128], 0)
             nc.vector.memset(xs[k][:].bitcast(I32).rearrange("p (g w) -> p g w", g=4)[:, :, 16:32], 0)
-        nc.vector.tensor_copy(out=tri[:], in_=tri_f[:].unsqueeze(1).to_broadcast([P, 4, P]))
+        nc.vector.tensor_copy(out=tri[:], in_=tri_f[:])
+        keep = tri[:].bitcast(I32)
+        for (shift, bits) in ((ALU.logical_shift_left, 2), (ALU.logical_shift_right, 7)):
+            nc.vector.tensor_single_scalar(out=spread[:], in_=keep, scalar=bits, op=shift)
+            nc.vector.tensor_tensor(out=keep, in0=keep, in1=spread[:], op=ALU.bitwise_or)
         nc.vector.tensor_copy(out=outb[:], in_=outb_raw[:])
 
         for b in range(XG_BUFS):
@@ -153,8 +158,9 @@ def tile_mixerblock_pa_t_kernel(tc, x_proj, mix_mat, mix_b, out_w, out_b, out):
             group_x_s(g)
             group_x_g(g)
             for j in range(4):
-                diag = wr[:, 4 * g:4 * g + 4, j, P * j:P * (j + 1)]
-                nc.vector.tensor_tensor(out=diag, in0=diag, in1=tri[:], op=ALU.mult)
+                diag = wr[:, 4 * g:4 * g + 4, j, P * j:P * (j + 1)].bitcast(I32)
+                nc.vector.tensor_tensor(out=diag, in0=diag, in1=keep.unsqueeze(1).to_broadcast([P, 4, P // 2]),
+                                        op=ALU.bitwise_and)
             for h in range(4 * g, 4 * g + 4):
                 wmg[h] = wgpool.tile([P, S, 4], BF16, name="wmg", tag="wmg", align_bytes=64)
                 group(nc.scalar.copy if h % 2 == 1 else nc.vector.tensor_copy, wmg[h][:], wr[:, h])

@@ -118,16 +118,16 @@ def tile_mixerblock_pa_t_kernel(tc, x_proj, mix_mat, mix_b, out_w, out_b, out):
             nc.vector.tensor_tensor(out=yg[b][:, cols, :], in0=ps1[(b, i)][:].rearrange("p j s -> p s j"),
                                     in1=bias_g[:, cols, :], op=ALU.add)
 
-        mb = mix_b.rearrange("(hp h2) s -> h2 hp s", h2=2)
-        for h2 in range(2):
-            nc.scalar.dma_start(out=bias_raw[64 * h2:64 * h2 + 64, :, :], in_=mb[h2].partition_broadcast(64))
-        nc.scalar.dma_start(out=outb_raw[:], in_=out_b.rearrange("(m r) -> m r", r=4))
         load_x(0)
         for j in range(4):
             load_w(0, j)
         load_x(1)
         for j in range(4):
             load_w(1, j)
+        mb = mix_b.rearrange("(hp h2) s -> h2 hp s", h2=2)
+        for h2 in range(2):
+            nc.sync.dma_start(out=bias_raw[64 * h2:64 * h2 + 64, :, :], in_=mb[h2].partition_broadcast(64))
+        nc.sync.dma_start(out=outb_raw[:], in_=out_b.rearrange("(m r) -> m r", r=4))
         load_x(2)
         nc.sync.dma_start(out=ow[:], in_=out_w.rearrange("(m r) c -> m r c", r=4))
         for b in range(3, XRAW_BUFS):
@@ -136,11 +136,12 @@ def tile_mixerblock_pa_t_kernel(tc, x_proj, mix_mat, mix_b, out_w, out_b, out):
         nc.gpsimd.memset(tri_f[:], 1.0)
         nc.gpsimd.affine_select(out=tri_f[:], in_=tri_f[:], pattern=[[1, P]], compare_op=ALU.is_ge,
                                 fill=0.0, base=0, channel_multiplier=-1)
+        for g in range(2):
+            for j in range(1, 4):
+                nc.gpsimd.memset(wr[:, 4 * g:4 * g + 4, j, 0:P * j], 0.0)
         make_identity(nc, ident[:])
         nc.gpsimd.tensor_scalar(out=bias_g[:], in0=bias_raw[:].rearrange("p j s -> p s j"), scalar1=1.0, scalar2=0.0,
                                 op0=ALU.mult, op1=ALU.add)
-        for j in range(1, 4):
-            nc.vector.memset(wr[:, :, j, 0:P * j], 0.0)
         for k in range(XQ_BUFS):
             nc.vector.memset(xq[k][:].bitcast(I32).rearrange("p (g w) -> p g w", g=4)[:, :, 64:128], 0)
             nc.vector.memset(xs[k][:].bitcast(I32).rearrange("p (g w) -> p g w", g=4)[:, :, 16:32], 0)
@@ -149,7 +150,6 @@ def tile_mixerblock_pa_t_kernel(tc, x_proj, mix_mat, mix_b, out_w, out_b, out):
         for (shift, bits) in ((ALU.logical_shift_left, 2), (ALU.logical_shift_right, 7)):
             nc.vector.tensor_single_scalar(out=spread[:], in_=keep, scalar=bits, op=shift)
             nc.vector.tensor_tensor(out=keep, in0=keep, in1=spread[:], op=ALU.bitwise_or)
-        nc.vector.tensor_copy(out=outb[:], in_=outb_raw[:])
 
         for b in range(XG_BUFS):
             new_xg_g(b)
@@ -168,6 +168,7 @@ def tile_mixerblock_pa_t_kernel(tc, x_proj, mix_mat, mix_b, out_w, out_b, out):
             for h in range(4 * g, 4 * g + 4):
                 nc.vector.quantize_mx(out=wq[:, h, :].bitcast(FP8X4), scales=ws[:, h, :],
                                       in_=wmg[h][:].rearrange("p s j -> p (s j)"))
+        nc.vector.tensor_copy(out=outb[:], in_=outb_raw[:])
         group_x_s(2)
         group_x_g(2)
         for r in range(4):

@@ -22,7 +22,7 @@ C_S = 192
 X_PIECES_S = ((0, 0, 64), (128, 64, 128))
 X_PIECES_G = ((320, 0, 128), (512, 128, 128), (704, 256, 64))
 XRAW_BUFS = 8
-XS_BUFS = 6
+XS_BUFS = 4
 XG_BUFS = 3
 
 
@@ -118,16 +118,16 @@ def tile_mixerblock_pa_t_kernel(tc, x_proj, mix_mat, mix_b, out_w, out_b, out):
             nc.vector.tensor_tensor(out=yg[b][:, cols, :], in0=ps1[(b, i)][:].rearrange("p j s -> p s j"),
                                     in1=bias_g[:, cols, :], op=ALU.add)
 
+        mb = mix_b.rearrange("(hp h2) s -> h2 hp s", h2=2)
+        for h2 in range(2):
+            nc.scalar.dma_start(out=bias_raw[64 * h2:64 * h2 + 64, :, :], in_=mb[h2].partition_broadcast(64))
+        nc.scalar.dma_start(out=outb_raw[:], in_=out_b.rearrange("(m r) -> m r", r=4))
         load_x(0)
         for j in range(4):
             load_w(0, j)
         load_x(1)
         for j in range(4):
             load_w(1, j)
-        mb = mix_b.rearrange("(hp h2) s -> h2 hp s", h2=2)
-        for h2 in range(2):
-            nc.sync.dma_start(out=bias_raw[64 * h2:64 * h2 + 64, :, :], in_=mb[h2].partition_broadcast(64))
-        nc.sync.dma_start(out=outb_raw[:], in_=out_b.rearrange("(m r) -> m r", r=4))
         load_x(2)
         nc.sync.dma_start(out=ow[:], in_=out_w.rearrange("(m r) c -> m r c", r=4))
         for b in range(3, XRAW_BUFS):
@@ -136,12 +136,11 @@ def tile_mixerblock_pa_t_kernel(tc, x_proj, mix_mat, mix_b, out_w, out_b, out):
         nc.gpsimd.memset(tri_f[:], 1.0)
         nc.gpsimd.affine_select(out=tri_f[:], in_=tri_f[:], pattern=[[1, P]], compare_op=ALU.is_ge,
                                 fill=0.0, base=0, channel_multiplier=-1)
-        for g in range(2):
-            for j in range(1, 4):
-                nc.gpsimd.memset(wr[:, 4 * g:4 * g + 4, j, 0:P * j], 0.0)
         make_identity(nc, ident[:])
         nc.gpsimd.tensor_scalar(out=bias_g[:], in0=bias_raw[:].rearrange("p j s -> p s j"), scalar1=1.0, scalar2=0.0,
                                 op0=ALU.mult, op1=ALU.add)
+        for j in range(1, 4):
+            nc.vector.memset(wr[:, :, j, 0:P * j], 0.0)
         for k in range(XQ_BUFS):
             nc.vector.memset(xq[k][:].bitcast(I32).rearrange("p (g w) -> p g w", g=4)[:, :, 64:128], 0)
             nc.vector.memset(xs[k][:].bitcast(I32).rearrange("p (g w) -> p g w", g=4)[:, :, 16:32], 0)
@@ -150,6 +149,7 @@ def tile_mixerblock_pa_t_kernel(tc, x_proj, mix_mat, mix_b, out_w, out_b, out):
         for (shift, bits) in ((ALU.logical_shift_left, 2), (ALU.logical_shift_right, 7)):
             nc.vector.tensor_single_scalar(out=spread[:], in_=keep, scalar=bits, op=shift)
             nc.vector.tensor_tensor(out=keep, in0=keep, in1=spread[:], op=ALU.bitwise_or)
+        nc.vector.tensor_copy(out=outb[:], in_=outb_raw[:])
 
         for b in range(XG_BUFS):
             new_xg_g(b)
@@ -168,7 +168,6 @@ def tile_mixerblock_pa_t_kernel(tc, x_proj, mix_mat, mix_b, out_w, out_b, out):
             for h in range(4 * g, 4 * g + 4):
                 nc.vector.quantize_mx(out=wq[:, h, :].bitcast(FP8X4), scales=ws[:, h, :],
                                       in_=wmg[h][:].rearrange("p s j -> p (s j)"))
-        nc.vector.tensor_copy(out=outb[:], in_=outb_raw[:])
         group_x_s(2)
         group_x_g(2)
         for r in range(4):
@@ -216,6 +215,6 @@ def tile_mixerblock_pa_t_kernel(tc, x_proj, mix_mat, mix_b, out_w, out_b, out):
                         nc.scalar.activation(out=ob[:, k, :], in_=ps2[:], func=ACT.Identity, bias=outb[:, r:r + 1],
                                              scale=1.0)
                         if last:
-                            nc.scalar.dma_start(out=rows[:, r:r + 1, :], in_=ob[:, k:k + 1, :])
+                            nc.sync.dma_start(out=rows[:, r:r + 1, :], in_=ob[:, k:k + 1, :])
                 if not last:
-                    nc.scalar.dma_start(out=rows[:, 2 * half:2 * half + 2, :], in_=ob[:])
+                    nc.sync.dma_start(out=rows[:, 2 * half:2 * half + 2, :], in_=ob[:])

@@ -23,7 +23,8 @@ X_PIECES_S = ((0, 0, 64), (128, 64, 128))
 X_PIECES_G = ((320, 0, 128), (512, 128, 128), (704, 256, 64))
 XRAW_BUFS = 8
 XS_BUFS = 4
-XG_BUFS = 3
+XG_BUFS = 2
+FIRST_G = 3
 
 
 def tile_mixerblock_pa_t_kernel(tc, x_proj, mix_mat, mix_b, out_w, out_b, out):
@@ -33,14 +34,15 @@ def tile_mixerblock_pa_t_kernel(tc, x_proj, mix_mat, mix_b, out_w, out_b, out):
         xpool = ctx.enter_context(tc.tile_pool(name="xraw", bufs=XRAW_BUFS))
         xspool = ctx.enter_context(tc.tile_pool(name="xgrouped_s", bufs=XS_BUFS))
         xgpool = ctx.enter_context(tc.tile_pool(name="xgrouped_g", bufs=XG_BUFS))
-        wgpool = ctx.enter_context(tc.tile_pool(name="wgrouped", bufs=4))
+        wgpool = ctx.enter_context(tc.tile_pool(name="wgrouped", bufs=H))
         ypool = ctx.enter_context(tc.tile_pool(name="y", bufs=3))
         opool = ctx.enter_context(tc.tile_pool(name="outs", bufs=6))
         psum1 = ctx.enter_context(tc.psum_pool(name="psum1", bufs=4))
         psum2 = ctx.enter_context(tc.psum_pool(name="psum2", bufs=4))
         ctx.enter_context(tc.manual_schedule())
 
-        bias_raw = const.tile([P, 4, S], BF16, name="bias_raw")
+        bias_rows = const.tile([P, S], BF16, name="bias_rows")
+        sel = const.tile([P, H, P // 2], BF16, name="sel")
         bias_g = const.tile([P, S, 4], BF16, name="bias_g")
         outb_raw = const.tile([P, 4], BF16, name="outb_raw")
         outb = const.tile([P, 4], F32, name="outb")
@@ -54,6 +56,7 @@ def tile_mixerblock_pa_t_kernel(tc, x_proj, mix_mat, mix_b, out_w, out_b, out):
         tri_f = const.tile([P, P], F32, name="tri_f")
         tri = const.tile([P, P], BF16, name="tri")
         spread = const.tile([P, P // 2], I32, name="spread")
+        zeros = const.tile([P, 3 * P], BF16, name="zeros")
         ident = const.tile([P, P], BF16, name="ident")
         xq = [const.tile([P, XQ_W], U32, name="xq%d" % k, align_bytes=64) for k in range(XQ_BUFS)]
         xs = [const.tile([P, XQ_W], U8, name="xs%d" % k, align_bytes=64) for k in range(XQ_BUFS)]
@@ -63,6 +66,7 @@ def tile_mixerblock_pa_t_kernel(tc, x_proj, mix_mat, mix_b, out_w, out_b, out):
         wmg = {}
         ps1 = {}
         yg = {}
+        psb = {}
 
         def load_x(b):
             xraw[b] = xpool.tile([P, 4, E], BF16, name="xr", tag="xr")
@@ -85,7 +89,7 @@ def tile_mixerblock_pa_t_kernel(tc, x_proj, mix_mat, mix_b, out_w, out_b, out):
         def group_x_g(b):
             if b >= XG_BUFS:
                 new_xg_g(b)
-            if b < XG_BUFS:
+            if b < FIRST_G:
                 group(nc.scalar.copy, xg_g[b][:], xraw[b][:, :, C_S:E])
             else:
                 nc.gpsimd.tensor_scalar(out=xg_g[b][:], in0=xraw[b][:, :, C_S:E].rearrange("p t c -> p c t"),
@@ -97,7 +101,7 @@ def tile_mixerblock_pa_t_kernel(tc, x_proj, mix_mat, mix_b, out_w, out_b, out):
                     nc.vector.quantize_mx(out=xq[b % XQ_BUFS][:, w0:w0 + n].bitcast(FP8X4),
                                           scales=xs[b % XQ_BUFS][:, w0:w0 + n],
                                           in_=src[:, c0:c0 + n, :].rearrange("p c j -> p (c j)"))
-            if b + XG_BUFS < B:
+            if FIRST_G <= b + XG_BUFS < B:
                 group_x_g(b + XG_BUFS)
 
         def mix(b, i):
@@ -118,13 +122,12 @@ def tile_mixerblock_pa_t_kernel(tc, x_proj, mix_mat, mix_b, out_w, out_b, out):
             nc.vector.tensor_tensor(out=yg[b][:, cols, :], in0=ps1[(b, i)][:].rearrange("p j s -> p s j"),
                                     in1=bias_g[:, cols, :], op=ALU.add)
 
-        mb = mix_b.rearrange("(hp h2) s -> h2 hp s", h2=2)
-        for h2 in range(2):
-            nc.scalar.dma_start(out=bias_raw[64 * h2:64 * h2 + 64, :, :], in_=mb[h2].partition_broadcast(64))
+        nc.gpsimd.memset(bias_rows[:].bitcast(I32), 0)
+        nc.scalar.dma_start(out=bias_rows[0:H, :], in_=mix_b)
         nc.scalar.dma_start(out=outb_raw[:], in_=out_b.rearrange("(m r) -> m r", r=4))
-        load_x(0)
         for j in range(4):
             load_w(0, j)
+        load_x(0)
         load_x(1)
         for j in range(4):
             load_w(1, j)
@@ -133,43 +136,68 @@ def tile_mixerblock_pa_t_kernel(tc, x_proj, mix_mat, mix_b, out_w, out_b, out):
         for b in range(3, XRAW_BUFS):
             load_x(b)
 
+        nc.vector.memset(zeros[:].bitcast(I32), 0)
+        nc.vector.memset(wr[:, 0:4, 1, 0:P], 0.0)
+        for j in range(2, 4):
+            nc.scalar.copy(out=wr[:, 0:4, j, 0:P * j], in_=zeros[:, 0:P * j].unsqueeze(1).to_broadcast([P, 4, P * j]))
         nc.gpsimd.memset(tri_f[:], 1.0)
         nc.gpsimd.affine_select(out=tri_f[:], in_=tri_f[:], pattern=[[1, P]], compare_op=ALU.is_ge,
                                 fill=0.0, base=0, channel_multiplier=-1)
         make_identity(nc, ident[:])
-        nc.gpsimd.tensor_scalar(out=bias_g[:], in0=bias_raw[:].rearrange("p j s -> p s j"), scalar1=1.0, scalar2=0.0,
-                                op0=ALU.mult, op1=ALU.add)
         for j in range(1, 4):
-            nc.vector.memset(wr[:, :, j, 0:P * j], 0.0)
+            nc.gpsimd.memset(wr[:, 4:8, j, 0:P * j], 0.0)
         for k in range(XQ_BUFS):
             nc.vector.memset(xq[k][:].bitcast(I32).rearrange("p (g w) -> p g w", g=4)[:, :, 64:128], 0)
             nc.vector.memset(xs[k][:].bitcast(I32).rearrange("p (g w) -> p g w", g=4)[:, :, 16:32], 0)
         nc.vector.tensor_copy(out=tri[:], in_=tri_f[:])
+        nc.vector.tensor_copy(out=sel[:], in_=ident[:, 0:H].unsqueeze(2).to_broadcast([P, H, P // 2]))
         keep = tri[:].bitcast(I32)
         for (shift, bits) in ((ALU.logical_shift_left, 2), (ALU.logical_shift_right, 7)):
             nc.vector.tensor_single_scalar(out=spread[:], in_=keep, scalar=bits, op=shift)
             nc.vector.tensor_tensor(out=keep, in0=keep, in1=spread[:], op=ALU.bitwise_or)
-        nc.vector.tensor_copy(out=outb[:], in_=outb_raw[:])
 
         for b in range(XG_BUFS):
             new_xg_g(b)
 
-        for g in range(2):
-            group_x_s(g)
-            group_x_g(g)
+        def mask_w(g):
             for j in range(4):
                 diag = wr[:, 4 * g:4 * g + 4, j, P * j:P * (j + 1)].bitcast(I32)
                 nc.vector.tensor_tensor(out=diag, in0=diag, in1=keep.unsqueeze(1).to_broadcast([P, 4, P // 2]),
                                         op=ALU.bitwise_and)
-            for h in range(4 * g, 4 * g + 4):
-                wmg[h] = wgpool.tile([P, S, 4], BF16, name="wmg", tag="wmg", align_bytes=64)
-                group(nc.scalar.copy if h % 2 == 1 else nc.vector.tensor_copy, wmg[h][:], wr[:, h])
-            quantise_x(g)
-            for h in range(4 * g, 4 * g + 4):
-                nc.vector.quantize_mx(out=wq[:, h, :].bitcast(FP8X4), scales=ws[:, h, :],
-                                      in_=wmg[h][:].rearrange("p s j -> p (s j)"))
-        group_x_s(2)
-        group_x_g(2)
+
+        def group_w(h):
+            wmg[h] = wgpool.tile([P, S, 4], BF16, name="wmg", tag="wmg", align_bytes=64)
+            group(nc.scalar.copy if h % 2 == 1 else nc.vector.tensor_copy, wmg[h][:], wr[:, h])
+
+        def quantise_w(h):
+            nc.vector.quantize_mx(out=wq[:, h, :].bitcast(FP8X4), scales=ws[:, h, :],
+                                  in_=wmg[h][:].rearrange("p s j -> p (s j)"))
+
+        for half in range(2):
+            psb[half] = psum2.tile([P, 4, 2 * P], BF16, name="psb", tag="s2")
+            for hp in range(4):
+                nc.tensor.matmul(psb[half][:, hp, :], lhsT=sel[:, 2 * hp:2 * hp + 2, :].rearrange("p h m -> p (h m)"),
+                                 rhs=bias_rows[:, 2 * P * half:2 * P * (half + 1)], start=True, stop=True)
+        group_x_s(0)
+        group_x_g(0)
+        mask_w(0)
+        for h in range(4):
+            group_w(h)
+        quantise_x(0)
+        quantise_w(0)
+        quantise_w(2)
+        mask_w(1)
+        for h in range(4, 8):
+            group_w(h)
+        for h in (1, 3, 4, 6, 5, 7):
+            quantise_w(h)
+        for half in range(2):
+            nc.scalar.copy(out=bias_g[:, 2 * P * half:2 * P * (half + 1), :], in_=psb[half][:].rearrange("p j s -> p s j"))
+        for i in range(4):
+            mix(0, i)
+        for b in range(1, 3):
+            group_x_s(b)
+            group_x_g(b)
         for r in range(4):
             pst = psum2.tile([P, 4, P], BF16, name="pst", tag="s2")
             for j in range(4):
@@ -177,8 +205,7 @@ def tile_mixerblock_pa_t_kernel(tc, x_proj, mix_mat, mix_b, out_w, out_b, out):
             nc.scalar.copy(out=owg[:, r, :, :], in_=pst[:].rearrange("p j m -> p m j"))
         for b in range(3, XS_BUFS):
             group_x_s(b)
-        for i in range(4):
-            mix(0, i)
+        nc.vector.tensor_copy(out=outb[:], in_=outb_raw[:])
 
         for b in range(B):
             if b + XRAW_BUFS < B:
@@ -188,8 +215,12 @@ def tile_mixerblock_pa_t_kernel(tc, x_proj, mix_mat, mix_b, out_w, out_b, out):
             yg[b] = ypool.tile([P, S, 4], BF16, name="yg", tag="yg", align_bytes=64)
             for i in range(4):
                 add_mix_bias(b, i)
-                if b + 1 < B:
+                if 0 < b < B - 1:
                     mix(b + 1, i)
+            if b == 0:
+                quantise_x(1)
+                for i in range(4):
+                    mix(1, i)
             if b + 2 < B:
                 quantise_x(b + 2)
             if b == 0:

@@ -18,13 +18,12 @@ FLOPS = 2 * 2 * B * S * S * E
 
 XQ_W = 768
 XQ_BUFS = 4
-C_S = 192
-X_PIECES_S = ((0, 0, 64), (128, 64, 128))
-X_PIECES_G = ((320, 0, 128), (512, 128, 128), (704, 256, 64))
+C_S = 320
+X_PIECES_S = ((0, 0, 64), (128, 64, 128), (320, 192, 128))
+X_PIECES_G = ((512, 0, 128), (704, 128, 64))
 XRAW_BUFS = 8
 XS_BUFS = 4
-XG_BUFS = 2
-FIRST_G = 3
+XG_BUFS = 3
 
 
 def tile_mixerblock_pa_t_kernel(tc, x_proj, mix_mat, mix_b, out_w, out_b, out):
@@ -83,17 +82,9 @@ def tile_mixerblock_pa_t_kernel(tc, x_proj, mix_mat, mix_b, out_w, out_b, out):
             xg_s[b] = xspool.tile([P, C_S, 4], BF16, name="xg_s", tag="xg_s", align_bytes=64)
             group(nc.scalar.copy, xg_s[b][:], xraw[b][:, :, 0:C_S])
 
-        def new_xg_g(b):
+        def group_x_v(b):
             xg_g[b] = xgpool.tile([P, E - C_S, 4], BF16, name="xg_g", tag="xg_g", align_bytes=64)
-
-        def group_x_g(b):
-            if b >= XG_BUFS:
-                new_xg_g(b)
-            if b < FIRST_G:
-                group(nc.scalar.copy, xg_g[b][:], xraw[b][:, :, C_S:E])
-            else:
-                nc.gpsimd.tensor_scalar(out=xg_g[b][:], in0=xraw[b][:, :, C_S:E].rearrange("p t c -> p c t"),
-                                        scalar1=1.0, scalar2=0.0, op0=ALU.mult, op1=ALU.add)
+            group(nc.vector.tensor_copy, xg_g[b][:], xraw[b][:, :, C_S:E])
 
         def quantise_x(b):
             for (pieces, src) in ((X_PIECES_S, xg_s[b]), (X_PIECES_G, xg_g[b])):
@@ -101,8 +92,6 @@ def tile_mixerblock_pa_t_kernel(tc, x_proj, mix_mat, mix_b, out_w, out_b, out):
                     nc.vector.quantize_mx(out=xq[b % XQ_BUFS][:, w0:w0 + n].bitcast(FP8X4),
                                           scales=xs[b % XQ_BUFS][:, w0:w0 + n],
                                           in_=src[:, c0:c0 + n, :].rearrange("p c j -> p (c j)"))
-            if FIRST_G <= b + XG_BUFS < B:
-                group_x_g(b + XG_BUFS)
 
         def mix(b, i):
             cols = slice(P * i, P * (i + 1))
@@ -156,9 +145,6 @@ def tile_mixerblock_pa_t_kernel(tc, x_proj, mix_mat, mix_b, out_w, out_b, out):
             nc.vector.tensor_single_scalar(out=spread[:], in_=keep, scalar=bits, op=shift)
             nc.vector.tensor_tensor(out=keep, in0=keep, in1=spread[:], op=ALU.bitwise_or)
 
-        for b in range(XG_BUFS):
-            new_xg_g(b)
-
         def mask_w(g):
             for j in range(4):
                 diag = wr[:, 4 * g:4 * g + 4, j, P * j:P * (j + 1)].bitcast(I32)
@@ -179,7 +165,7 @@ def tile_mixerblock_pa_t_kernel(tc, x_proj, mix_mat, mix_b, out_w, out_b, out):
                 nc.tensor.matmul(psb[half][:, hp, :], lhsT=sel[:, 2 * hp:2 * hp + 2, :].rearrange("p h m -> p (h m)"),
                                  rhs=bias_rows[:, 2 * P * half:2 * P * (half + 1)], start=True, stop=True)
         group_x_s(0)
-        group_x_g(0)
+        group_x_v(0)
         mask_w(0)
         for h in range(4):
             group_w(h)
@@ -197,7 +183,6 @@ def tile_mixerblock_pa_t_kernel(tc, x_proj, mix_mat, mix_b, out_w, out_b, out):
             mix(0, i)
         for b in range(1, 3):
             group_x_s(b)
-            group_x_g(b)
         for r in range(4):
             pst = psum2.tile([P, 4, P], BF16, name="pst", tag="s2")
             for j in range(4):
@@ -218,9 +203,13 @@ def tile_mixerblock_pa_t_kernel(tc, x_proj, mix_mat, mix_b, out_w, out_b, out):
                 if 0 < b < B - 1:
                     mix(b + 1, i)
             if b == 0:
+                group_x_v(1)
+                group_x_v(2)
                 quantise_x(1)
                 for i in range(4):
                     mix(1, i)
+            if b + 3 < B:
+                group_x_v(b + 3)
             if b + 2 < B:
                 quantise_x(b + 2)
             if b == 0:

@@ -42,7 +42,7 @@ def tile_mixerblock_pa_t_kernel(tc, x_proj, mix_mat, mix_b, out_w, out_b, out):
 
         bias_rows = const.tile([P, S], BF16, name="bias_rows")
         sel = const.tile([P, H, P // 2], BF16, name="sel")
-        bias_g = const.tile([P, S, 4], BF16, name="bias_g")
+        bias_g = const.tile([P, 4, S], BF16, name="bias_g")
         outb_raw = const.tile([P, 4], BF16, name="outb_raw")
         outb = const.tile([P, 4], F32, name="outb")
         wr = const.tile([P, H, 4, S], BF16, name="wr")
@@ -108,8 +108,9 @@ def tile_mixerblock_pa_t_kernel(tc, x_proj, mix_mat, mix_b, out_w, out_b, out):
 
         def add_mix_bias(b, i):
             cols = slice(P * i, P * (i + 1))
-            nc.vector.tensor_tensor(out=yg[b][:, cols, :], in0=ps1[(b, i)][:].rearrange("p j s -> p s j"),
-                                    in1=bias_g[:, cols, :], op=ALU.add)
+            nc.vector.tensor_tensor(out=yg[b][:, cols, :].rearrange("p (c i) t -> p c t i", i=4),
+                                    in0=ps1[(b, i)][:].rearrange("p t (c i) -> p c t i", i=4),
+                                    in1=bias_g[:, :, cols].rearrange("p t (c i) -> p c t i", i=4), op=ALU.add)
 
         nc.gpsimd.memset(bias_rows[:].bitcast(I32), 0)
         nc.scalar.dma_start(out=bias_rows[0:H, :], in_=mix_b)
@@ -178,7 +179,7 @@ def tile_mixerblock_pa_t_kernel(tc, x_proj, mix_mat, mix_b, out_w, out_b, out):
         for h in (1, 3, 4, 6, 5, 7):
             quantise_w(h)
         for half in range(2):
-            nc.scalar.copy(out=bias_g[:, 2 * P * half:2 * P * (half + 1), :], in_=psb[half][:].rearrange("p j s -> p s j"))
+            nc.scalar.copy(out=bias_g[:, :, 2 * P * half:2 * P * (half + 1)], in_=psb[half][:])
         for i in range(4):
             mix(0, i)
         for b in range(1, 3):

@@ -14,6 +14,8 @@ ACT = mybir.ActivationFunctionType
 
 P = 128
 B, S, E, H = 16, 512, 512, 8
+T = S // P
+SH = S // 2
 FLOPS = 2 * 2 * B * S * S * E
 
 XQ_W = 768
@@ -23,7 +25,8 @@ X_PIECES_S = ((0, 0, 64), (128, 64, 128), (320, 192, 128))
 X_PIECES_G = ((512, 0, 128), (704, 128, 64))
 XRAW_BUFS = 8
 XS_BUFS = 4
-XG_BUFS = 3
+XG_BUFS = 2
+FIRST_G = 4
 
 
 def tile_mixerblock_pa_t_kernel(tc, x_proj, mix_mat, mix_b, out_w, out_b, out):
@@ -33,7 +36,6 @@ def tile_mixerblock_pa_t_kernel(tc, x_proj, mix_mat, mix_b, out_w, out_b, out):
         xpool = ctx.enter_context(tc.tile_pool(name="xraw", bufs=XRAW_BUFS))
         xspool = ctx.enter_context(tc.tile_pool(name="xgrouped_s", bufs=XS_BUFS))
         xgpool = ctx.enter_context(tc.tile_pool(name="xgrouped_g", bufs=XG_BUFS))
-        wgpool = ctx.enter_context(tc.tile_pool(name="wgrouped", bufs=H))
         ypool = ctx.enter_context(tc.tile_pool(name="y", bufs=3))
         opool = ctx.enter_context(tc.tile_pool(name="outs", bufs=6))
         psum1 = ctx.enter_context(tc.psum_pool(name="psum1", bufs=4))
@@ -45,9 +47,10 @@ def tile_mixerblock_pa_t_kernel(tc, x_proj, mix_mat, mix_b, out_w, out_b, out):
         bias_g = const.tile([P, 4, S], BF16, name="bias_g")
         outb_raw = const.tile([P, 4], BF16, name="outb_raw")
         outb = const.tile([P, 4], F32, name="outb")
-        wr = const.tile([P, H, 4, S], BF16, name="wr")
-        wq = const.tile([P, H, S], U32, name="wq", align_bytes=64)
-        ws = const.tile([P, H, S], U8, name="ws", align_bytes=64)
+        wr = [const.tile([P, H, 2 * (u + 1), SH], BF16, name="wr%d" % u) for u in range(2)]
+        wmg = [const.tile([P, H, P, 4], BF16, name="wmg%d" % i, align_bytes=64) for i in range(T)]
+        wq = const.tile([P, T, H, P], U32, name="wq", align_bytes=64)
+        ws = const.tile([P, T, H, P], U8, name="ws", align_bytes=64)
         ow = const.tile([P, 4, E], BF16, name="ow")
         owg = const.tile([P, 4, P, 4], BF16, name="owg", align_bytes=64)
         owq = const.tile([P, 4 * P], U32, name="owq", align_bytes=64)
@@ -55,25 +58,26 @@ def tile_mixerblock_pa_t_kernel(tc, x_proj, mix_mat, mix_b, out_w, out_b, out):
         tri_f = const.tile([P, P], F32, name="tri_f")
         tri = const.tile([P, P], BF16, name="tri")
         spread = const.tile([P, P // 2], I32, name="spread")
-        zeros = const.tile([P, 3 * P], BF16, name="zeros")
+        zero = const.tile([P, 8], U32, name="zero")
         ident = const.tile([P, P], BF16, name="ident")
         xq = [const.tile([P, XQ_W], U32, name="xq%d" % k, align_bytes=64) for k in range(XQ_BUFS)]
         xs = [const.tile([P, XQ_W], U8, name="xs%d" % k, align_bytes=64) for k in range(XQ_BUFS)]
         xraw = {}
         xg_s = {}
         xg_g = {}
-        wmg = {}
         ps1 = {}
-        yg = {}
         psb = {}
+        pst = {}
+        yg = {}
 
         def load_x(b):
             xraw[b] = xpool.tile([P, 4, E], BF16, name="xr", tag="xr")
             nc.sync.dma_start(out=xraw[b][:], in_=x_proj[b].rearrange("(j p) c -> p j c", p=P))
 
-        def load_w(g, j):
-            nc.sync.dma_start(out=wr[:, 4 * g:4 * g + 4, j, P * j:S],
-                              in_=mix_mat[4 * g:4 * g + 4, P * j:P * (j + 1), P * j:S].rearrange("h p s -> p h s"))
+        def load_w(u, j):
+            lo = max(P * j, SH * u)
+            nc.sync.dma_start(out=wr[u][:, :, j, lo - SH * u:SH],
+                              in_=mix_mat[:, P * j:P * (j + 1), lo:SH * (u + 1)].rearrange("h p s -> p h s"))
 
         def group(engine_copy, dst, src):
             engine_copy(out=dst.rearrange("p (c i) t -> p c t i", i=4), in_=src.rearrange("p t (c i) -> p c t i", i=4))
@@ -82,19 +86,47 @@ def tile_mixerblock_pa_t_kernel(tc, x_proj, mix_mat, mix_b, out_w, out_b, out):
             xg_s[b] = xspool.tile([P, C_S, 4], BF16, name="xg_s", tag="xg_s", align_bytes=64)
             group(nc.scalar.copy, xg_s[b][:], xraw[b][:, :, 0:C_S])
 
-        def group_x_v(b):
+        def group_x_g(b):
             xg_g[b] = xgpool.tile([P, E - C_S, 4], BF16, name="xg_g", tag="xg_g", align_bytes=64)
-            group(nc.vector.tensor_copy, xg_g[b][:], xraw[b][:, :, C_S:E])
+            if b < FIRST_G:
+                group(nc.vector.tensor_copy, xg_g[b][:], xraw[b][:, :, C_S:E])
+            else:
+                nc.gpsimd.tensor_scalar(out=xg_g[b][:], in0=xraw[b][:, :, C_S:E].rearrange("p t c -> p c t"),
+                                        scalar1=1.0, scalar2=0.0, op0=ALU.mult, op1=ALU.add)
 
-        def quantise_x(b):
-            for (pieces, src) in ((X_PIECES_S, xg_s[b]), (X_PIECES_G, xg_g[b])):
-                for (w0, c0, n) in pieces:
-                    nc.vector.quantize_mx(out=xq[b % XQ_BUFS][:, w0:w0 + n].bitcast(FP8X4),
-                                          scales=xs[b % XQ_BUFS][:, w0:w0 + n],
-                                          in_=src[:, c0:c0 + n, :].rearrange("p c j -> p (c j)"))
+        def quantise_x(b, pieces, src):
+            for (w0, c0, n) in pieces:
+                nc.vector.quantize_mx(out=xq[b % XQ_BUFS][:, w0:w0 + n].bitcast(FP8X4),
+                                      scales=xs[b % XQ_BUFS][:, w0:w0 + n],
+                                      in_=src[:, c0:c0 + n, :].rearrange("p c j -> p (c j)"))
+
+        def quantise_x_s(b):
+            quantise_x(b, X_PIECES_S, xg_s[b])
+
+        def quantise_x_g(b):
+            quantise_x(b, X_PIECES_G, xg_g[b])
+            if FIRST_G <= b + XG_BUFS < B:
+                group_x_g(b + XG_BUFS)
+
+        def mask_w(i):
+            cols = slice(P * (i % 2), P * (i % 2) + P)
+            diag = wr[i // 2][:, :, i, cols].bitcast(I32)
+            nc.vector.tensor_tensor(out=diag, in0=diag, in1=keep.unsqueeze(1).to_broadcast([P, H, P // 2]),
+                                    op=ALU.bitwise_and)
+
+        def group_w(i):
+            cols = slice(P * (i % 2), P * (i % 2) + P)
+            for (engine_copy, heads) in ((nc.vector.tensor_copy, slice(0, 4)), (nc.scalar.copy, slice(4, 8))):
+                engine_copy(out=wmg[i][:, heads, :, 0:i + 1],
+                            in_=wr[i // 2][:, heads, 0:i + 1, cols].rearrange("p h t s -> p h s t"))
+
+        def quantise_w(i):
+            for heads in (slice(0, 4), slice(4, 8)):
+                nc.vector.quantize_mx(out=wq[:, i, heads, :].rearrange("p h s -> p (h s)").bitcast(FP8X4),
+                                      scales=ws[:, i, heads, :].rearrange("p h s -> p (h s)"),
+                                      in_=wmg[i][:, heads, :, :].rearrange("p h s t -> p (h s t)"))
 
         def mix(b, i):
-            cols = slice(P * i, P * (i + 1))
             ps1[(b, i)] = psum1.tile([P, 4, P], F32, name="ps1", tag="s1")
             for hp in range(4):
                 for h2 in range(2):
@@ -102,9 +134,12 @@ def tile_mixerblock_pa_t_kernel(tc, x_proj, mix_mat, mix_b, out_w, out_b, out):
                     nc.tensor.matmul_mx(out=ps1[(b, i)][:, hp, :],
                                         lhsT=xq[b % XQ_BUFS][:, w0:w0 + P].bitcast(FP8X4),
                                         lhsT_scale=xs[b % XQ_BUFS][:, w0:w0 + P],
-                                        rhs=wq[:, 2 * hp + h2, cols].bitcast(FP8X4),
-                                        rhs_scale=ws[:, 2 * hp + h2, cols],
+                                        rhs=wq[:, i, 2 * hp + h2, :].bitcast(FP8X4),
+                                        rhs_scale=ws[:, i, 2 * hp + h2, :],
                                         start=(h2 == 0), stop=(h2 == 1))
+
+        def new_y(b):
+            yg[b] = ypool.tile([P, S, 4], BF16, name="yg", tag="yg", align_bytes=64)
 
         def add_mix_bias(b, i):
             cols = slice(P * i, P * (i + 1))
@@ -112,130 +147,147 @@ def tile_mixerblock_pa_t_kernel(tc, x_proj, mix_mat, mix_b, out_w, out_b, out):
                                     in0=ps1[(b, i)][:].rearrange("p t (c i) -> p c t i", i=4),
                                     in1=bias_g[:, :, cols].rearrange("p t (c i) -> p c t i", i=4), op=ALU.add)
 
-        nc.gpsimd.memset(bias_rows[:].bitcast(I32), 0)
-        nc.scalar.dma_start(out=bias_rows[0:H, :], in_=mix_b)
-        nc.scalar.dma_start(out=outb_raw[:], in_=out_b.rearrange("(m r) -> m r", r=4))
-        for j in range(4):
-            load_w(0, j)
-        load_x(0)
-        load_x(1)
-        for j in range(4):
-            load_w(1, j)
-        load_x(2)
-        nc.sync.dma_start(out=ow[:], in_=out_w.rearrange("(m r) c -> m r c", r=4))
-        for b in range(3, XRAW_BUFS):
-            load_x(b)
-
-        nc.vector.memset(zeros[:].bitcast(I32), 0)
-        nc.vector.memset(wr[:, 0:4, 1, 0:P], 0.0)
-        for j in range(2, 4):
-            nc.scalar.copy(out=wr[:, 0:4, j, 0:P * j], in_=zeros[:, 0:P * j].unsqueeze(1).to_broadcast([P, 4, P * j]))
-        nc.gpsimd.memset(tri_f[:], 1.0)
-        nc.gpsimd.affine_select(out=tri_f[:], in_=tri_f[:], pattern=[[1, P]], compare_op=ALU.is_ge,
-                                fill=0.0, base=0, channel_multiplier=-1)
-        make_identity(nc, ident[:])
-        for j in range(1, 4):
-            nc.gpsimd.memset(wr[:, 4:8, j, 0:P * j], 0.0)
-        for k in range(XQ_BUFS):
-            nc.vector.memset(xq[k][:].bitcast(I32).rearrange("p (g w) -> p g w", g=4)[:, :, 64:128], 0)
-            nc.vector.memset(xs[k][:].bitcast(I32).rearrange("p (g w) -> p g w", g=4)[:, :, 16:32], 0)
-        nc.vector.tensor_copy(out=tri[:], in_=tri_f[:])
-        nc.vector.tensor_copy(out=sel[:], in_=ident[:, 0:H].unsqueeze(2).to_broadcast([P, H, P // 2]))
-        keep = tri[:].bitcast(I32)
-        for (shift, bits) in ((ALU.logical_shift_left, 2), (ALU.logical_shift_right, 7)):
-            nc.vector.tensor_single_scalar(out=spread[:], in_=keep, scalar=bits, op=shift)
-            nc.vector.tensor_tensor(out=keep, in0=keep, in1=spread[:], op=ALU.bitwise_or)
-
-        def mask_w(g):
-            for j in range(4):
-                diag = wr[:, 4 * g:4 * g + 4, j, P * j:P * (j + 1)].bitcast(I32)
-                nc.vector.tensor_tensor(out=diag, in0=diag, in1=keep.unsqueeze(1).to_broadcast([P, 4, P // 2]),
-                                        op=ALU.bitwise_and)
-
-        def group_w(h):
-            wmg[h] = wgpool.tile([P, S, 4], BF16, name="wmg", tag="wmg", align_bytes=64)
-            group(nc.scalar.copy if h % 2 == 1 else nc.vector.tensor_copy, wmg[h][:], wr[:, h])
-
-        def quantise_w(h):
-            nc.vector.quantize_mx(out=wq[:, h, :].bitcast(FP8X4), scales=ws[:, h, :],
-                                  in_=wmg[h][:].rearrange("p s j -> p (s j)"))
-
-        for half in range(2):
-            psb[half] = psum2.tile([P, 4, 2 * P], BF16, name="psb", tag="s2")
-            for hp in range(4):
-                nc.tensor.matmul(psb[half][:, hp, :], lhsT=sel[:, 2 * hp:2 * hp + 2, :].rearrange("p h m -> p (h m)"),
-                                 rhs=bias_rows[:, 2 * P * half:2 * P * (half + 1)], start=True, stop=True)
-        group_x_s(0)
-        group_x_v(0)
-        mask_w(0)
-        for h in range(4):
-            group_w(h)
-        quantise_x(0)
-        quantise_w(0)
-        quantise_w(2)
-        mask_w(1)
-        for h in range(4, 8):
-            group_w(h)
-        for h in (1, 3, 4, 6, 5, 7):
-            quantise_w(h)
-        for half in range(2):
-            nc.scalar.copy(out=bias_g[:, :, 2 * P * half:2 * P * (half + 1)], in_=psb[half][:])
-        for i in range(4):
-            mix(0, i)
-        for b in range(1, 3):
-            group_x_s(b)
-        for r in range(4):
-            pst = psum2.tile([P, 4, P], BF16, name="pst", tag="s2")
-            for j in range(4):
-                nc.tensor.transpose(pst[:, j, :], ow[:, r, P * j:P * (j + 1)], ident[:])
-            nc.scalar.copy(out=owg[:, r, :, :], in_=pst[:].rearrange("p j m -> p m j"))
-        for b in range(3, XS_BUFS):
-            group_x_s(b)
-        nc.vector.tensor_copy(out=outb[:], in_=outb_raw[:])
-
-        for b in range(B):
-            if b + XRAW_BUFS < B:
-                load_x(b + XRAW_BUFS)
-            if b + XS_BUFS < B:
-                group_x_s(b + XS_BUFS)
-            yg[b] = ypool.tile([P, S, 4], BF16, name="yg", tag="yg", align_bytes=64)
-            for i in range(4):
-                add_mix_bias(b, i)
-                if 0 < b < B - 1:
-                    mix(b + 1, i)
-            if b == 0:
-                group_x_v(1)
-                group_x_v(2)
-                quantise_x(1)
-                for i in range(4):
-                    mix(1, i)
-            if b + 3 < B:
-                group_x_v(b + 3)
-            if b + 2 < B:
-                quantise_x(b + 2)
-            if b == 0:
-                nc.vector.quantize_mx(out=owq[:].bitcast(FP8X4), scales=ows[:],
-                                      in_=owg[:].rearrange("p r m j -> p (r m j)"))
+        def quantise_y(b, lo, n):
             yq = ypool.tile([P, S], U32, name="yq", tag="yq", align_bytes=64)
             ys = ypool.tile([P, S], U8, name="ys", tag="ys", align_bytes=64)
-            nc.vector.quantize_mx(out=yq[:].bitcast(FP8X4), scales=ys[:], in_=yg[b][:].rearrange("p s j -> p (s j)"))
+            nc.vector.quantize_mx(out=yq[:, 0:n].bitcast(FP8X4), scales=ys[:, 0:n],
+                                  in_=yg[b][:, lo:lo + n, :].rearrange("p s j -> p (s j)"))
+            return (yq, ys)
+
+        def project(b, y, lo, n, vector_rows):
+            (yq, ys) = y
             rows = out[b].rearrange("(m r) s -> m r s", r=4)
-            last = b == B - 1
             for half in range(2):
                 ob = opool.tile([P, 2, S], F32, name="ob", tag="ob")
                 for k in range(2):
                     r = 2 * half + k
                     ps2 = psum2.tile([P, S], F32, name="ps2", tag="s2")
-                    nc.tensor.matmul_mx(out=ps2[:], lhsT=owq[:, P * r:P * (r + 1)].bitcast(FP8X4),
+                    nc.tensor.matmul_mx(out=ps2[:, 0:n], lhsT=owq[:, P * r:P * (r + 1)].bitcast(FP8X4),
                                         lhsT_scale=ows[:, P * r:P * (r + 1)],
-                                        rhs=yq[:].bitcast(FP8X4), rhs_scale=ys[:], start=True, stop=True)
-                    if last and k == 1:
-                        nc.vector.tensor_scalar_add(out=ob[:, k, :], in0=ps2[:], scalar1=outb[:, r:r + 1])
-                        nc.sync.dma_start(out=rows[:, r:r + 1, :], in_=ob[:, k:k + 1, :])
+                                        rhs=yq[:, 0:n].bitcast(FP8X4), rhs_scale=ys[:, 0:n], start=True, stop=True)
+                    if r in vector_rows:
+                        nc.vector.tensor_scalar_add(out=ob[:, k, 0:n], in0=ps2[:, 0:n], scalar1=outb[:, r:r + 1])
                     else:
-                        nc.scalar.activation(out=ob[:, k, :], in_=ps2[:], func=ACT.Identity, bias=outb[:, r:r + 1],
-                                             scale=1.0)
-                        if last:
-                            nc.sync.dma_start(out=rows[:, r:r + 1, :], in_=ob[:, k:k + 1, :])
-                if not last:
-                    nc.sync.dma_start(out=rows[:, 2 * half:2 * half + 2, :], in_=ob[:])
+                        nc.scalar.activation(out=ob[:, k, 0:n], in_=ps2[:, 0:n], func=ACT.Identity,
+                                             bias=outb[:, r:r + 1], scale=1.0)
+                nc.sync.dma_start(out=rows[:, 2 * half:2 * half + 2, lo:lo + n], in_=ob[:, :, 0:n])
+
+        nc.gpsimd.memset(bias_rows[:].bitcast(I32), 0)
+        nc.scalar.dma_start(out=bias_rows[0:H, :], in_=mix_b)
+        nc.scalar.dma_start(out=outb_raw[:], in_=out_b.rearrange("(m r) -> m r", r=4))
+        for j in range(2):
+            load_w(0, j)
+        load_x(0)
+        for j in range(4):
+            load_w(1, j)
+        load_x(1)
+        load_x(2)
+        nc.sync.dma_start(out=ow[:], in_=out_w.rearrange("(m r) c -> m r c", r=4))
+        for b in range(3, XRAW_BUFS):
+            load_x(b)
+
+        nc.vector.memset(zero[:], 0)
+        nc.scalar.copy(out=wmg[2][:].rearrange("p h s t -> p (h s t)").bitcast(U32),
+                       in_=zero[:, 0:1].to_broadcast([P, H * P * 2]))
+        nc.gpsimd.memset(tri_f[:], 1.0)
+        nc.gpsimd.affine_select(out=tri_f[:], in_=tri_f[:], pattern=[[1, P]], compare_op=ALU.is_ge,
+                                fill=0.0, base=0, channel_multiplier=-1)
+        make_identity(nc, ident[:])
+        nc.gpsimd.memset(wmg[1][:].rearrange("p h s t -> p (h s t)").bitcast(I32), 0)
+        nc.vector.memset(wmg[0][:].rearrange("p h s t -> p (h s t)").bitcast(I32), 0)
+        for k in range(XQ_BUFS):
+            nc.gpsimd.memset(xq[k][:].bitcast(I32).rearrange("p (g w) -> p g w", g=4)[:, :, 64:128], 0)
+            nc.gpsimd.memset(xs[k][:].bitcast(I32).rearrange("p (g w) -> p g w", g=4)[:, :, 16:32], 0)
+        nc.vector.tensor_copy(out=tri[:], in_=tri_f[:])
+        keep = tri[:].bitcast(I32)
+        for (shift, bits) in ((ALU.logical_shift_left, 2), (ALU.logical_shift_right, 7)):
+            nc.vector.tensor_single_scalar(out=spread[:], in_=keep, scalar=bits, op=shift)
+            nc.vector.tensor_tensor(out=keep, in0=keep, in1=spread[:], op=ALU.bitwise_or)
+
+        for i in range(2):
+            mask_w(i)
+        nc.vector.tensor_copy(out=sel[:], in_=ident[:, 0:H].unsqueeze(2).to_broadcast([P, H, P // 2]))
+        for half in range(2):
+            psb[half] = psum2.tile([P, 4, SH], BF16, name="psb", tag="s2")
+            for hp in range(4):
+                nc.tensor.matmul(psb[half][:, hp, :], lhsT=sel[:, 2 * hp:2 * hp + 2, :].rearrange("p h m -> p (h m)"),
+                                 rhs=bias_rows[:, SH * half:SH * (half + 1)], start=True, stop=True)
+        group_x_s(0)
+        group_x_g(0)
+        for i in range(2):
+            group_w(i)
+        quantise_x_s(0)
+        quantise_x_g(0)
+        for i in range(2):
+            quantise_w(i)
+        for half in range(2):
+            nc.scalar.copy(out=bias_g[:, :, SH * half:SH * (half + 1)], in_=psb[half][:])
+        for i in range(2):
+            mix(0, i)
+        for r in range(4):
+            pst[r] = psum2.tile([P, 4, P], BF16, name="pst", tag="s2")
+            for j in range(4):
+                nc.tensor.transpose(pst[r][:, j, :], ow[:, r, P * j:P * (j + 1)], ident[:])
+        for i in range(2, 4):
+            mask_w(i)
+        new_y(0)
+        for i in range(2):
+            add_mix_bias(0, i)
+        group_x_s(1)
+        group_x_g(1)
+        for i in range(2, 4):
+            group_w(i)
+        quantise_x_s(1)
+        quantise_x_g(1)
+        for i in range(2):
+            mix(1, i)
+        for i in range(2, 4):
+            quantise_w(i)
+        for i in range(2, 4):
+            mix(0, i)
+        new_y(1)
+        for i in range(2):
+            add_mix_bias(1, i)
+        group_x_s(2)
+        group_x_g(2)
+        for i in range(2, 4):
+            add_mix_bias(0, i)
+        for i in range(2, 4):
+            mix(1, i)
+        for r in range(4):
+            nc.scalar.copy(out=owg[:, r, :, :], in_=pst[r][:].rearrange("p j m -> p m j"))
+        nc.vector.tensor_copy(out=outb[:], in_=outb_raw[:])
+        group_x_g(3)
+        quantise_x_s(2)
+        y = quantise_y(0, 0, S)
+        quantise_x_g(2)
+        nc.vector.quantize_mx(out=owq[:].bitcast(FP8X4), scales=ows[:], in_=owg[:].rearrange("p r m j -> p (r m j)"))
+        group_x_s(3)
+        project(0, y, 0, S, ())
+
+        for b in range(1, B - 1):
+            if b + XRAW_BUFS - 1 < B:
+                load_x(b + XRAW_BUFS - 1)
+            if b + 3 < B:
+                group_x_s(b + 3)
+            if b == 1:
+                for i in range(2):
+                    mix(2, i)
+            else:
+                new_y(b)
+            for i in range(2 if b == 1 else 0, 4):
+                add_mix_bias(b, i)
+                mix(b + 1, i)
+            if b + 2 < B:
+                quantise_x_s(b + 2)
+            y = quantise_y(b, 0, S)
+            if b + 2 < B:
+                quantise_x_g(b + 2)
+            project(b, y, 0, S, ())
+
+        new_y(B - 1)
+        for half in range(2):
+            for i in (2 * half, 2 * half + 1):
+                add_mix_bias(B - 1, i)
+            y = quantise_y(B - 1, SH * half, SH)
+            project(B - 1, y, SH * half, SH, (1, 3) if half == 1 else ())

@@ -20,9 +20,9 @@ FLOPS = 2 * 2 * B * S * S * E
 
 XQ_W = 768
 XQ_BUFS = 4
-C_S = 320
-X_PIECES_S = ((0, 0, 64), (128, 64, 128), (320, 192, 128))
-X_PIECES_G = ((512, 0, 128), (704, 128, 64))
+C_S = 192
+X_PIECES_S = ((0, 0, 64), (128, 64, 128))
+X_PIECES_G = ((320, 0, 128), (512, 128, 128), (704, 256, 64))
 XRAW_BUFS = 8
 XS_BUFS = 4
 XG_BUFS = 2

@@ -48,20 +48,20 @@ def tile_mixerblock_pa_t_kernel(tc, x_proj, mix_mat, mix_b, out_w, out_b, out):
         outb_raw = const.tile([P, 4], BF16, name="outb_raw")
         outb = const.tile([P, 4], F32, name="outb")
         wr = [const.tile([P, H, 2 * (u + 1), SH], BF16, name="wr%d" % u) for u in range(2)]
-        wmg = [const.tile([P, H, P, 4], BF16, name="wmg%d" % i, align_bytes=64) for i in range(T)]
-        wq = const.tile([P, T, H, P], U32, name="wq", align_bytes=64)
-        ws = const.tile([P, T, H, P], U8, name="ws", align_bytes=64)
+        wmg = [const.tile([P, H, P, 4], BF16, name="wmg%d" % i, align_bytes=256) for i in range(T)]
+        wq = const.tile([P, T, H, P], U32, name="wq", align_bytes=256)
+        ws = const.tile([P, T, H, P], U8, name="ws", align_bytes=256)
         ow = const.tile([P, 4, E], BF16, name="ow")
-        owg = const.tile([P, 4, P, 4], BF16, name="owg", align_bytes=64)
-        owq = const.tile([P, 4 * P], U32, name="owq", align_bytes=64)
-        ows = const.tile([P, 4 * P], U8, name="ows", align_bytes=64)
+        owg = const.tile([P, 4, P, 4], BF16, name="owg", align_bytes=256)
+        owq = const.tile([P, 4 * P], U32, name="owq", align_bytes=256)
+        ows = const.tile([P, 4 * P], U8, name="ows", align_bytes=256)
         tri_f = const.tile([P, P], F32, name="tri_f")
         tri = const.tile([P, P], BF16, name="tri")
         spread = const.tile([P, P // 2], I32, name="spread")
         zero = const.tile([P, 8], U32, name="zero")
         ident = const.tile([P, P], BF16, name="ident")
-        xq = [const.tile([P, XQ_W], U32, name="xq%d" % k, align_bytes=64) for k in range(XQ_BUFS)]
-        xs = [const.tile([P, XQ_W], U8, name="xs%d" % k, align_bytes=64) for k in range(XQ_BUFS)]
+        xq = [const.tile([P, XQ_W], U32, name="xq%d" % k, align_bytes=256) for k in range(XQ_BUFS)]
+        xs = [const.tile([P, XQ_W], U8, name="xs%d" % k, align_bytes=256) for k in range(XQ_BUFS)]
         xraw = {}
         xg_s = {}
         xg_g = {}
@@ -83,13 +83,13 @@ def tile_mixerblock_pa_t_kernel(tc, x_proj, mix_mat, mix_b, out_w, out_b, out):
             engine_copy(out=dst.rearrange("p (c i) t -> p c t i", i=4), in_=src.rearrange("p t (c i) -> p c t i", i=4))
 
         def group_x_s(b):
-            xg_s[b] = xspool.tile([P, C_S, 4], BF16, name="xg_s", tag="xg_s", align_bytes=64)
+            xg_s[b] = xspool.tile([P, C_S, 4], BF16, name="xg_s", tag="xg_s", align_bytes=256)
             group(nc.scalar.copy, xg_s[b][:], xraw[b][:, :, 0:C_S])
 
         def group_x_g(b):
-            xg_g[b] = xgpool.tile([P, E - C_S, 4], BF16, name="xg_g", tag="xg_g", align_bytes=64)
+            xg_g[b] = xgpool.tile([P, E - C_S, 4], BF16, name="xg_g", tag="xg_g", align_bytes=256)
             if b < FIRST_G:
-                group(nc.vector.tensor_copy, xg_g[b][:], xraw[b][:, :, C_S:E])
+                group(nc.vector.tensor_copy if b == 0 else nc.scalar.copy, xg_g[b][:], xraw[b][:, :, C_S:E])
             else:
                 nc.gpsimd.tensor_scalar(out=xg_g[b][:], in0=xraw[b][:, :, C_S:E].rearrange("p t c -> p c t"),
                                         scalar1=1.0, scalar2=0.0, op0=ALU.mult, op1=ALU.add)
@@ -126,20 +126,23 @@ def tile_mixerblock_pa_t_kernel(tc, x_proj, mix_mat, mix_b, out_w, out_b, out):
                                       scales=ws[:, i, heads, :].rearrange("p h s -> p (h s)"),
                                       in_=wmg[i][:, heads, :, :].rearrange("p h s t -> p (h s t)"))
 
-        def mix(b, i):
-            ps1[(b, i)] = psum1.tile([P, 4, P], F32, name="ps1", tag="s1")
+        def mix(b, half):
+            tiles = (2 * half, 2 * half + 1)
+            for i in tiles:
+                ps1[(b, i)] = psum1.tile([P, 4, P], F32, name="ps1", tag="s1")
             for hp in range(4):
                 for h2 in range(2):
                     w0 = 192 * hp + 64 * h2
-                    nc.tensor.matmul_mx(out=ps1[(b, i)][:, hp, :],
-                                        lhsT=xq[b % XQ_BUFS][:, w0:w0 + P].bitcast(FP8X4),
-                                        lhsT_scale=xs[b % XQ_BUFS][:, w0:w0 + P],
-                                        rhs=wq[:, i, 2 * hp + h2, :].bitcast(FP8X4),
-                                        rhs_scale=ws[:, i, 2 * hp + h2, :],
-                                        start=(h2 == 0), stop=(h2 == 1))
+                    for i in tiles:
+                        nc.tensor.matmul_mx(out=ps1[(b, i)][:, hp, :],
+                                            lhsT=xq[b % XQ_BUFS][:, w0:w0 + P].bitcast(FP8X4),
+                                            lhsT_scale=xs[b % XQ_BUFS][:, w0:w0 + P],
+                                            rhs=wq[:, i, 2 * hp + h2, :].bitcast(FP8X4),
+                                            rhs_scale=ws[:, i, 2 * hp + h2, :],
+                                            start=(h2 == 0), stop=(h2 == 1))
 
         def new_y(b):
-            yg[b] = ypool.tile([P, S, 4], BF16, name="yg", tag="yg", align_bytes=64)
+            yg[b] = ypool.tile([P, S, 4], BF16, name="yg", tag="yg", align_bytes=256)
 
         def add_mix_bias(b, i):
             cols = slice(P * i, P * (i + 1))
@@ -148,8 +151,8 @@ def tile_mixerblock_pa_t_kernel(tc, x_proj, mix_mat, mix_b, out_w, out_b, out):
                                     in1=bias_g[:, :, cols].rearrange("p t (c i) -> p c t i", i=4), op=ALU.add)
 
         def quantise_y(b, lo, n):
-            yq = ypool.tile([P, S], U32, name="yq", tag="yq", align_bytes=64)
-            ys = ypool.tile([P, S], U8, name="ys", tag="ys", align_bytes=64)
+            yq = ypool.tile([P, S], U32, name="yq", tag="yq", align_bytes=256)
+            ys = ypool.tile([P, S], U8, name="ys", tag="ys", align_bytes=256)
             nc.vector.quantize_mx(out=yq[:, 0:n].bitcast(FP8X4), scales=ys[:, 0:n],
                                   in_=yg[b][:, lo:lo + n, :].rearrange("p s j -> p (s j)"))
             return (yq, ys)
@@ -222,8 +225,7 @@ def tile_mixerblock_pa_t_kernel(tc, x_proj, mix_mat, mix_b, out_w, out_b, out):
             quantise_w(i)
         for half in range(2):
             nc.scalar.copy(out=bias_g[:, :, SH * half:SH * (half + 1)], in_=psb[half][:])
-        for i in range(2):
-            mix(0, i)
+        mix(0, 0)
         for r in range(4):
             pst[r] = psum2.tile([P, 4, P], BF16, name="pst", tag="s2")
             for j in range(4):
@@ -239,12 +241,10 @@ def tile_mixerblock_pa_t_kernel(tc, x_proj, mix_mat, mix_b, out_w, out_b, out):
             group_w(i)
         quantise_x_s(1)
         quantise_x_g(1)
-        for i in range(2):
-            mix(1, i)
+        mix(1, 0)
         for i in range(2, 4):
             quantise_w(i)
-        for i in range(2, 4):
-            mix(0, i)
+        mix(0, 1)
         new_y(1)
         for i in range(2):
             add_mix_bias(1, i)
@@ -252,8 +252,7 @@ def tile_mixerblock_pa_t_kernel(tc, x_proj, mix_mat, mix_b, out_w, out_b, out):
         group_x_g(2)
         for i in range(2, 4):
             add_mix_bias(0, i)
-        for i in range(2, 4):
-            mix(1, i)
+        mix(1, 1)
         for r in range(4):
             nc.scalar.copy(out=owg[:, r, :, :], in_=pst[r][:].rearrange("p j m -> p m j"))
         nc.vector.tensor_copy(out=outb[:], in_=outb_raw[:])
@@ -271,13 +270,13 @@ def tile_mixerblock_pa_t_kernel(tc, x_proj, mix_mat, mix_b, out_w, out_b, out):
             if b + 3 < B:
                 group_x_s(b + 3)
             if b == 1:
-                for i in range(2):
-                    mix(2, i)
+                mix(2, 0)
             else:
                 new_y(b)
-            for i in range(2 if b == 1 else 0, 4):
-                add_mix_bias(b, i)
-                mix(b + 1, i)
+            for half in range(1 if b == 1 else 0, 2):
+                for i in (2 * half, 2 * half + 1):
+                    add_mix_bias(b, i)
+                mix(b + 1, half)
             if b + 2 < B:
                 quantise_x_s(b + 2)
             y = quantise_y(b, 0, S)

from contextlib import ExitStack

import concourse.mybir as mybir
from concourse.masks import make_identity

BF16 = mybir.dt.bfloat16
F32 = mybir.dt.float32
I32 = mybir.dt.int32
U32 = mybir.dt.uint32
U8 = mybir.dt.uint8
FP8X4 = mybir.dt.float8_e4m3fn_x4
ALU = mybir.AluOpType
ACT = mybir.ActivationFunctionType

P = 128
B, S, E, H = 16, 512, 512, 8
T = S // P
SH = S // 2
FLOPS = 2 * 2 * B * S * S * E

XQ_W = 768
XQ_BUFS = 4
C_S = 192
X_PIECES_S = ((0, 0, 64), (128, 64, 128))
X_PIECES_G = ((320, 0, 128), (512, 128, 128), (704, 256, 64))
XRAW_BUFS = 8
XS_BUFS = 4
XG_BUFS = 2
FIRST_G = 4


def tile_mixerblock_pa_t_kernel(tc, x_proj, mix_mat, mix_b, out_w, out_b, out):
    nc = tc.nc
    with ExitStack() as ctx:
        const = ctx.enter_context(tc.tile_pool(name="const", bufs=1))
        xpool = ctx.enter_context(tc.tile_pool(name="xraw", bufs=XRAW_BUFS))
        xspool = ctx.enter_context(tc.tile_pool(name="xgrouped_s", bufs=XS_BUFS))
        xgpool = ctx.enter_context(tc.tile_pool(name="xgrouped_g", bufs=XG_BUFS))
        ypool = ctx.enter_context(tc.tile_pool(name="y", bufs=3))
        opool = ctx.enter_context(tc.tile_pool(name="outs", bufs=6))
        psum1 = ctx.enter_context(tc.psum_pool(name="psum1", bufs=4))
        psum2 = ctx.enter_context(tc.psum_pool(name="psum2", bufs=4))
        ctx.enter_context(tc.manual_schedule())

        bias_rows = const.tile([P, S], BF16, name="bias_rows")
        sel = const.tile([P, H, P // 2], BF16, name="sel")
        bias_g = const.tile([P, 4, S], BF16, name="bias_g")
        outb_raw = const.tile([P, 4], BF16, name="outb_raw")
        outb = const.tile([P, 4], F32, name="outb")
        wr = [const.tile([P, H, 2 * (u + 1), SH], BF16, name="wr%d" % u) for u in range(2)]
        wmg = [const.tile([P, H, P, 4], BF16, name="wmg%d" % i, align_bytes=256) for i in range(T)]
        wq = const.tile([P, T, H, P], U32, name="wq", align_bytes=256)
        ws = const.tile([P, T, H, P], U8, name="ws", align_bytes=256)
        ow = const.tile([P, 4, E], BF16, name="ow")
        owg = const.tile([P, 4, P, 4], BF16, name="owg", align_bytes=256)
        owq = const.tile([P, 4 * P], U32, name="owq", align_bytes=256)
        ows = const.tile([P, 4 * P], U8, name="ows", align_bytes=256)
        tri_f = const.tile([P, P], F32, name="tri_f")
        tri = const.tile([P, P], BF16, name="tri")
        spread = const.tile([P, P // 2], I32, name="spread")
        zero = const.tile([P, 8], U32, name="zero")
        ident = const.tile([P, P], BF16, name="ident")
        xq = [const.tile([P, XQ_W], U32, name="xq%d" % k, align_bytes=256) for k in range(XQ_BUFS)]
        xs = [const.tile([P, XQ_W], U8, name="xs%d" % k, align_bytes=256) for k in range(XQ_BUFS)]
        xraw = {}
        xg_s = {}
        xg_g = {}
        ps1 = {}
        psb = {}
        pst = {}
        yg = {}

        def load_x(b):
            xraw[b] = xpool.tile([P, 4, E], BF16, name="xr", tag="xr")
            nc.sync.dma_start(out=xraw[b][:], in_=x_proj[b].rearrange("(j p) c -> p j c", p=P))

        def load_w(u, j):
            lo = max(P * j, SH * u)
            nc.sync.dma_start(out=wr[u][:, :, j, lo - SH * u:SH],
                              in_=mix_mat[:, P * j:P * (j + 1), lo:SH * (u + 1)].rearrange("h p s -> p h s"))

        def group(engine_copy, dst, src):
            engine_copy(out=dst.rearrange("p (c i) t -> p c t i", i=4), in_=src.rearrange("p t (c i) -> p c t i", i=4))

        def group_x_s(b):
            xg_s[b] = xspool.tile([P, C_S, 4], BF16, name="xg_s", tag="xg_s", align_bytes=256)
            group(nc.scalar.copy, xg_s[b][:], xraw[b][:, :, 0:C_S])

        def group_x_g(b):
            xg_g[b] = xgpool.tile([P, E - C_S, 4], BF16, name="xg_g", tag="xg_g", align_bytes=256)
            if b < FIRST_G:
                group(nc.vector.tensor_copy if b == 0 else nc.scalar.copy, xg_g[b][:], xraw[b][:, :, C_S:E])
            else:
                nc.gpsimd.tensor_scalar(out=xg_g[b][:], in0=xraw[b][:, :, C_S:E].rearrange("p t c -> p c t"),
                                        scalar1=1.0, scalar2=0.0, op0=ALU.mult, op1=ALU.add)

        def quantise_x(b, pieces, src):
            for (w0, c0, n) in pieces:
                nc.vector.quantize_mx(out=xq[b % XQ_BUFS][:, w0:w0 + n].bitcast(FP8X4),
                                      scales=xs[b % XQ_BUFS][:, w0:w0 + n],
                                      in_=src[:, c0:c0 + n, :].rearrange("p c j -> p (c j)"))

        def quantise_x_s(b):
            quantise_x(b, X_PIECES_S, xg_s[b])

        def quantise_x_g(b):
            quantise_x(b, X_PIECES_G, xg_g[b])
            if FIRST_G <= b + XG_BUFS < B:
                group_x_g(b + XG_BUFS)

        def mask_w(i):
            cols = slice(P * (i % 2), P * (i % 2) + P)
            diag = wr[i // 2][:, :, i, cols].bitcast(I32)
            nc.vector.tensor_tensor(out=diag, in0=diag, in1=keep.unsqueeze(1).to_broadcast([P, H, P // 2]),
                                    op=ALU.bitwise_and)

        def group_w(i):
            cols = slice(P * (i % 2), P * (i % 2) + P)
            for (engine_copy, heads) in ((nc.vector.tensor_copy, slice(0, 4)), (nc.scalar.copy, slice(4, 8))):
                engine_copy(out=wmg[i][:, heads, :, 0:i + 1],
                            in_=wr[i // 2][:, heads, 0:i + 1, cols].rearrange("p h t s -> p h s t"))

        def quantise_w(i):
            for heads in (slice(0, 4), slice(4, 8)):
                nc.vector.quantize_mx(out=wq[:, i, heads, :].rearrange("p h s -> p (h s)").bitcast(FP8X4),
                                      scales=ws[:, i, heads, :].rearrange("p h s -> p (h s)"),
                                      in_=wmg[i][:, heads, :, :].rearrange("p h s t -> p (h s t)"))

        def mix(b, half):
            tiles = (2 * half, 2 * half + 1)
            for i in tiles:
                ps1[(b, i)] = psum1.tile([P, 4, P], F32, name="ps1", tag="s1")
            for hp in range(4):
                for h2 in range(2):
                    w0 = 192 * hp + 64 * h2
                    for i in tiles:
                        nc.tensor.matmul_mx(out=ps1[(b, i)][:, hp, :],
                                            lhsT=xq[b % XQ_BUFS][:, w0:w0 + P].bitcast(FP8X4),
                                            lhsT_scale=xs[b % XQ_BUFS][:, w0:w0 + P],
                                            rhs=wq[:, i, 2 * hp + h2, :].bitcast(FP8X4),
                                            rhs_scale=ws[:, i, 2 * hp + h2, :],
                                            start=(h2 == 0), stop=(h2 == 1))

        def new_y(b):
            yg[b] = ypool.tile([P, S, 4], BF16, name="yg", tag="yg", align_bytes=256)

        def add_mix_bias(b, i):
            cols = slice(P * i, P * (i + 1))
            nc.vector.tensor_tensor(out=yg[b][:, cols, :].rearrange("p (c i) t -> p c t i", i=4),
                                    in0=ps1[(b, i)][:].rearrange("p t (c i) -> p c t i", i=4),
                                    in1=bias_g[:, :, cols].rearrange("p t (c i) -> p c t i", i=4), op=ALU.add)

        def quantise_y(b, lo, n):
            yq = ypool.tile([P, S], U32, name="yq", tag="yq", align_bytes=256)
            ys = ypool.tile([P, S], U8, name="ys", tag="ys", align_bytes=256)
            nc.vector.quantize_mx(out=yq[:, 0:n].bitcast(FP8X4), scales=ys[:, 0:n],
                                  in_=yg[b][:, lo:lo + n, :].rearrange("p s j -> p (s j)"))
            return (yq, ys)

        def project(b, y, lo, n, vector_rows):
            (yq, ys) = y
            rows = out[b].rearrange("(m r) s -> m r s", r=4)
            for half in range(2):
                ob = opool.tile([P, 2, S], F32, name="ob", tag="ob")
                for k in range(2):
                    r = 2 * half + k
                    ps2 = psum2.tile([P, S], F32, name="ps2", tag="s2")
                    nc.tensor.matmul_mx(out=ps2[:, 0:n], lhsT=owq[:, P * r:P * (r + 1)].bitcast(FP8X4),
                                        lhsT_scale=ows[:, P * r:P * (r + 1)],
                                        rhs=yq[:, 0:n].bitcast(FP8X4), rhs_scale=ys[:, 0:n], start=True, stop=True)
                    if r in vector_rows:
                        nc.vector.tensor_scalar_add(out=ob[:, k, 0:n], in0=ps2[:, 0:n], scalar1=outb[:, r:r + 1])
                    else:
                        nc.scalar.activation(out=ob[:, k, 0:n], in_=ps2[:, 0:n], func=ACT.Identity,
                                             bias=outb[:, r:r + 1], scale=1.0)
                nc.sync.dma_start(out=rows[:, 2 * half:2 * half + 2, lo:lo + n], in_=ob[:, :, 0:n])

        nc.gpsimd.memset(bias_rows[:].bitcast(I32), 0)
        nc.scalar.dma_start(out=bias_rows[0:H, :], in_=mix_b)
        nc.scalar.dma_start(out=outb_raw[:], in_=out_b.rearrange("(m r) -> m r", r=4))
        for j in range(2):
            load_w(0, j)
        load_x(0)
        for j in range(4):
            load_w(1, j)
        load_x(1)
        load_x(2)
        nc.sync.dma_start(out=ow[:], in_=out_w.rearrange("(m r) c -> m r c", r=4))
        for b in range(3, XRAW_BUFS):
            load_x(b)

        nc.vector.memset(zero[:], 0)
        nc.scalar.copy(out=wmg[2][:].rearrange("p h s t -> p (h s t)").bitcast(U32),
                       in_=zero[:, 0:1].to_broadcast([P, H * P * 2]))
        nc.gpsimd.memset(tri_f[:], 1.0)
        nc.gpsimd.affine_select(out=tri_f[:], in_=tri_f[:], pattern=[[1, P]], compare_op=ALU.is_ge,
                                fill=0.0, base=0, channel_multiplier=-1)
        make_identity(nc, ident[:])
        nc.gpsimd.memset(wmg[1][:].rearrange("p h s t -> p (h s t)").bitcast(I32), 0)
        nc.vector.memset(wmg[0][:].rearrange("p h s t -> p (h s t)").bitcast(I32), 0)
        for k in range(XQ_BUFS):
            nc.gpsimd.memset(xq[k][:].bitcast(I32).rearrange("p (g w) -> p g w", g=4)[:, :, 64:128], 0)
            nc.gpsimd.memset(xs[k][:].bitcast(I32).rearrange("p (g w) -> p g w", g=4)[:, :, 16:32], 0)
        nc.vector.tensor_copy(out=tri[:], in_=tri_f[:])
        keep = tri[:].bitcast(I32)
        for (shift, bits) in ((ALU.logical_shift_left, 2), (ALU.logical_shift_right, 7)):
            nc.vector.tensor_single_scalar(out=spread[:], in_=keep, scalar=bits, op=shift)
            nc.vector.tensor_tensor(out=keep, in0=keep, in1=spread[:], op=ALU.bitwise_or)

        for i in range(2):
            mask_w(i)
        nc.vector.tensor_copy(out=sel[:], in_=ident[:, 0:H].unsqueeze(2).to_broadcast([P, H, P // 2]))
        for half in range(2):
            psb[half] = psum2.tile([P, 4, SH], BF16, name="psb", tag="s2")
            for hp in range(4):
                nc.tensor.matmul(psb[half][:, hp, :], lhsT=sel[:, 2 * hp:2 * hp + 2, :].rearrange("p h m -> p (h m)"),
                                 rhs=bias_rows[:, SH * half:SH * (half + 1)], start=True, stop=True)
        group_x_s(0)
        group_x_g(0)
        for i in range(2):
            group_w(i)
        quantise_x_s(0)
        quantise_x_g(0)
        for i in range(2):
            quantise_w(i)
        for half in range(2):
            nc.scalar.copy(out=bias_g[:, :, SH * half:SH * (half + 1)], in_=psb[half][:])
        mix(0, 0)
        for r in range(4):
            pst[r] = psum2.tile([P, 4, P], BF16, name="pst", tag="s2")
            for j in range(4):
                nc.tensor.transpose(pst[r][:, j, :], ow[:, r, P * j:P * (j + 1)], ident[:])
        for i in range(2, 4):
            mask_w(i)
        new_y(0)
        for i in range(2):
            add_mix_bias(0, i)
        group_x_s(1)
        group_x_g(1)
        for i in range(2, 4):
            group_w(i)
        quantise_x_s(1)
        quantise_x_g(1)
        mix(1, 0)
        for i in range(2, 4):
            quantise_w(i)
        mix(0, 1)
        new_y(1)
        for i in range(2):
            add_mix_bias(1, i)
        group_x_s(2)
        group_x_g(2)
        for i in range(2, 4):
            add_mix_bias(0, i)
        mix(1, 1)
        for r in range(4):
            nc.scalar.copy(out=owg[:, r, :, :], in_=pst[r][:].rearrange("p j m -> p m j"))
        nc.vector.tensor_copy(out=outb[:], in_=outb_raw[:])
        group_x_g(3)
        quantise_x_s(2)
        y = quantise_y(0, 0, S)
        quantise_x_g(2)
        nc.vector.quantize_mx(out=owq[:].bitcast(FP8X4), scales=ows[:], in_=owg[:].rearrange("p r m j -> p (r m j)"))
        group_x_s(3)
        project(0, y, 0, S, ())

        for b in range(1, B - 1):
            if b + XRAW_BUFS - 1 < B:
                load_x(b + XRAW_BUFS - 1)
            if b + 3 < B:
                group_x_s(b + 3)
            if b == 1:
                mix(2, 0)
            else:
                new_y(b)
            for half in range(1 if b == 1 else 0, 2):
                for i in (2 * half, 2 * half + 1):
                    add_mix_bias(b, i)
                mix(b + 1, half)
            if b + 2 < B:
                quantise_x_s(b + 2)
            y = quantise_y(b, 0, S)
            if b + 2 < B:
                quantise_x_g(b + 2)
            project(b, y, 0, S, ())

        new_y(B - 1)
        for half in range(2):
            for i in (2 * half, 2 * half + 1):
                add_mix_bias(B - 1, i)
            y = quantise_y(B - 1, SH * half, SH)
            project(B - 1, y, SH * half, SH, (1, 3) if half == 1 else ())
